import numpy as np
import ml_dtypes


def mxq(x, axis, fmt="e4m3"):
    dtype, down = {"e4m3": (ml_dtypes.float8_e4m3fn, 7), "e5m2": (ml_dtypes.float8_e5m2, 14)}[fmt]
    v = np.moveaxis(np.asarray(x, np.float32).astype(ml_dtypes.bfloat16).astype(np.float64), axis, -1)
    blocks = v.reshape(v.shape[:-1] + (-1, 32))
    amax = np.abs(blocks).max(-1, keepdims=True)
    byte = np.maximum(np.where(amax > 0, np.frexp(amax)[1] - 1 + 127, 0) - down, 1)
    scale = np.exp2(byte - 127.0)
    codes = (blocks / scale).astype(np.float32).astype(dtype).astype(np.float64)
    return np.moveaxis((codes * scale).reshape(v.shape), -1, axis)


WIDE = False


def mx_kscale(k):
    if not WIDE:
        return np.ones(k)
    levels = np.array([10, -10, 5, -5, 0])
    a = np.random.permutation(np.resize(levels, k // 512 * 4)).reshape(k // 512, 4)
    idx = np.arange(k)
    return np.exp2(a[idx // 512, idx % 128 // 32])


BF16 = ml_dtypes.bfloat16


def bf(x):
    return np.asarray(x, np.float32).astype(BF16)


def f64(x):
    return np.asarray(x).astype(np.float64)


B, D, H = 512, 2048, 1024


def sigmoid(v):
    return 1.0 / (1.0 + np.exp(-v))


def setup_inputs():
    s = mx_kscale(H)

    def act(a):
        return np.random.standard_normal((B, H)) * a

    def wgt():
        return np.random.standard_normal((H, H)) * 0.7 / np.sqrt(H)

    return {"xz_i": bf(act(0.7)), "xz_f": bf(act(0.7)), "xz_g": bf(act(0.7)),
            "h_prev": bf(act(1.0) * s), "c_prev": bf(act(1.0)),
            "w_hi": bf(wgt() / s[:, None]), "w_ci": bf(wgt()),
            "w_hf": bf(wgt() / s[:, None]), "w_cf": bf(wgt()),
            "w_hg": bf(wgt() / s[:, None]),
            "b_i": bf(np.random.standard_normal(H) * 0.3), "b_f": bf(np.random.standard_normal(H) * 0.3), "b_g": bf(np.random.standard_normal(H) * 0.3)}


def reference(xz_i, xz_f, xz_g, h_prev, c_prev, w_hi, w_ci, w_hf, w_cf, w_hg, b_i, b_f, b_g):
    cp = f64(c_prev)
    hq = mxq(f64(h_prev), 1, "e4m3")
    cq = mxq(cp, 1, "e4m3")
    i = f64(xz_i) + (hq @ mxq(f64(w_hi), 0, "e4m3")) + (cq @ mxq(f64(w_ci), 0, "e4m3")) + f64(b_i)
    f = f64(xz_f) + (hq @ mxq(f64(w_hf), 0, "e4m3")) + (cq @ mxq(f64(w_cf), 0, "e4m3")) + f64(b_f)
    g = f64(xz_g) + (hq @ mxq(f64(w_hg), 0, "e4m3")) + f64(b_g)
    return sigmoid(f) * cp + sigmoid(i) * np.tanh(g)

@@ -1,0 +1,200 @@
+from contextlib import ExitStack
+
+import concourse.mybir as mybir
+from concourse.masks import make_identity
+
+F32 = mybir.dt.float32
+BF16 = mybir.dt.bfloat16
+U32 = mybir.dt.uint32
+U8 = mybir.dt.uint8
+FP8X4 = mybir.dt.float8_e4m3fn_x4
+ACT = mybir.ActivationFunctionType
+ALU = mybir.AluOpType
+
+P = 128
+PACK = 4
+K_PASS = P * PACK
+B = 512
+H = 1024
+M_TILES = B // P
+PASSES = H // K_PASS
+BANK = 512
+CH = 256
+CHUNKS = H // CH
+M_PER_BANK = BANK // CH
+BANKS = M_TILES // M_PER_BANK
+HALF = H // 2
+
+FLOPS = 2 * B * H * H * 5
+
+
+def tile_residuallstmcell_pa_kernel(
+    tc, xz_i, xz_f, xz_g, h_prev, c_prev, w_hi, w_ci, w_hf, w_cf, w_hg, b_i, b_f, b_g, out
+):
+    nc = tc.nc
+    with ExitStack() as stack:
+        keep = stack.enter_context(tc.tile_pool(name="keep", bufs=1))
+        regroup = stack.enter_context(tc.tile_pool(name="regroup", bufs=6))
+        quantised = stack.enter_context(tc.tile_pool(name="quantised", bufs=8))
+        work = stack.enter_context(tc.tile_pool(name="work", bufs=14))
+        psum_turn = stack.enter_context(tc.psum_pool(name="psum_turn", bufs=2))
+        psum_acc = stack.enter_context(tc.psum_pool(name="psum_acc", bufs=6))
+
+        ident = keep.tile([P, P], F32, name="ident")
+        make_identity(nc, ident[:])
+        warm = keep.tile([P, 1], F32, name="warm")
+        nc.vector.memset(warm[:], 0.0)
+        nc.scalar.activation(out=warm[:], in_=warm[:], func=ACT.Sigmoid)
+
+        def load_rows(name, src):
+            rows = keep.tile([P, M_TILES, H], BF16, name=name)
+            nc.sync.dma_start(out=rows[:], in_=src.rearrange("(m p) n -> p m n", p=P))
+            return rows
+
+        def load_weight_half(raw, w, half):
+            cols = slice(half * HALF, (half + 1) * HALF)
+            for g in range(PASSES):
+                nc.sync.dma_start(
+                    out=raw[:, g, :, cols],
+                    in_=w[g * K_PASS : (g + 1) * K_PASS, cols].rearrange("(p j) n -> p j n", j=PACK),
+                )
+
+        def load_bias(name, b):
+            spread = keep.tile([P, H], BF16, name=name)
+            nc.sync.dma_start(out=spread[:], in_=b.partition_broadcast(P))
+            return spread
+
+        raw_hg = keep.tile([P, PASSES, PACK, H], BF16, name="raw_hg")
+        raw_hi = keep.tile([P, PASSES, PACK, H], BF16, name="raw_hi")
+        raw_ci = keep.tile([P, PASSES, PACK, H], BF16, name="raw_ci")
+        raw_hf = keep.tile([P, PASSES, PACK, H], BF16, name="raw_hf")
+        raw_cf = keep.tile([P, PASSES, PACK, H], BF16, name="raw_cf")
+
+        load_weight_half(raw_hg, w_hg, 0)
+        h_sb = load_rows("h_sb", h_prev)
+        load_weight_half(raw_hg, w_hg, 1)
+        bias_g = load_bias("bias_g", b_g)
+        xz_g_sb = load_rows("xz_g_sb", xz_g)
+        c_sb = load_rows("c_sb", c_prev)
+        load_weight_half(raw_hi, w_hi, 0)
+        load_weight_half(raw_ci, w_ci, 0)
+        bias_i = load_bias("bias_i", b_i)
+        xz_i_sb = load_rows("xz_i_sb", xz_i)
+        load_weight_half(raw_hi, w_hi, 1)
+        load_weight_half(raw_ci, w_ci, 1)
+        load_weight_half(raw_hf, w_hf, 0)
+        load_weight_half(raw_cf, w_cf, 0)
+        bias_f = load_bias("bias_f", b_f)
+        xz_f_sb = load_rows("xz_f_sb", xz_f)
+        load_weight_half(raw_hf, w_hf, 1)
+        load_weight_half(raw_cf, w_cf, 1)
+
+        def quantise_activation(name, x_sb):
+            codes = keep.tile([P, M_TILES * PASSES * P], U32, name=name + "_codes", align_bytes=64)
+            scales = keep.tile([P, M_TILES * PASSES * P], U8, name=name + "_scales", align_bytes=64)
+            for m in range(M_TILES):
+                words = x_sb[:, m, :].bitcast(F32).rearrange("p (g q u) -> p g u q", g=PASSES, u=2)
+                turned = psum_turn.tile([P, PASSES, 2, P], F32, name="turned")
+                for g in range(PASSES):
+                    for u in range(2):
+                        nc.tensor.transpose(turned[:, g, u, :], words[:, g, u, :], ident[:])
+                x_grouped = regroup.tile(
+                    [P, PASSES, P, PACK], BF16, name="x_grouped", bufs=2, align_bytes=64
+                )
+                nc.vector.tensor_copy(
+                    out=x_grouped[:].bitcast(F32), in_=turned[:].rearrange("p g u b -> p g b u")
+                )
+                span = slice(m * PASSES * P, (m + 1) * PASSES * P)
+                nc.vector.quantize_mx(
+                    out=codes[:, span].bitcast(FP8X4),
+                    scales=scales[:, span],
+                    in_=x_grouped[:].rearrange("p g b t -> p (g b t)"),
+                )
+            return codes, scales
+
+        def quantise_weight_chunk(raw, chunk):
+            w_grouped = regroup.tile([P, PASSES, CH, PACK], BF16, name="w_grouped", align_bytes=64)
+            for g in range(PASSES):
+                src = raw[:, g, :, chunk * CH : (chunk + 1) * CH].rearrange("p t (c i) -> p c t i", i=4)
+                dst = w_grouped[:, g].rearrange("p (c i) t -> p c t i", i=4)
+                nc.scalar.copy(out=dst, in_=src)
+            w_codes = quantised.tile([P, PASSES * CH], U32, name="w_codes", align_bytes=64)
+            w_scales = quantised.tile([P, PASSES * CH], U8, name="w_scales", align_bytes=64)
+            nc.vector.quantize_mx(
+                out=w_codes[:].bitcast(FP8X4),
+                scales=w_scales[:],
+                in_=w_grouped[:].rearrange("p g c t -> p (g c t)"),
+            )
+            return w_codes, w_scales
+
+        cell = keep.tile([P, M_TILES, H], F32, name="cell")
+        out_rows = out.rearrange("(m p) n -> p m n", p=P)
+
+        def gate_chunk(gate, xz_sb, bias, products, chunk):
+            cols = slice(chunk * CH, (chunk + 1) * CH)
+            operands = []
+            for x_codes, x_scales, raw in products:
+                w_codes, w_scales = quantise_weight_chunk(raw, chunk)
+                for g in range(PASSES):
+                    operands.append((x_codes, x_scales, w_codes, w_scales, g))
+
+            rows_of = [slice(k * M_PER_BANK, (k + 1) * M_PER_BANK) for k in range(BANKS)]
+            pre = []
+            for k in range(BANKS):
+                pre_k = work.tile([P, M_PER_BANK, CH], F32, name="pre")
+                nc.vector.tensor_tensor(
+                    out=pre_k[:],
+                    in0=xz_sb[:, rows_of[k], cols],
+                    in1=bias[:, cols].unsqueeze(1).to_broadcast([P, M_PER_BANK, CH]),
+                    op=ALU.add,
+                )
+                pre.append(pre_k)
+
+            for k in range(BANKS):
+                acc = psum_acc.tile([P, M_PER_BANK, CH], F32, name="acc")
+                for s in range(M_PER_BANK):
+                    m = k * M_PER_BANK + s
+                    for step, (x_codes, x_scales, w_codes, w_scales, g) in enumerate(operands):
+                        x_cols = slice((m * PASSES + g) * P, (m * PASSES + g + 1) * P)
+                        w_cols = slice(g * CH, (g + 1) * CH)
+                        nc.tensor.matmul_mx(
+                            out=acc[:, s, :],
+                            lhsT=x_codes[:, x_cols].bitcast(FP8X4),
+                            lhsT_scale=x_scales[:, x_cols],
+                            rhs=w_codes[:, w_cols].bitcast(FP8X4),
+                            rhs_scale=w_scales[:, w_cols],
+                            start=(step == 0),
+                            stop=(step == len(operands) - 1),
+                        )
+                nc.vector.tensor_tensor(out=pre[k][:], in0=acc[:], in1=pre[k][:], op=ALU.add)
+
+            if gate == "g":
+                for k in range(BANKS):
+                    nc.scalar.activation(out=cell[:, rows_of[k], cols], in_=pre[k][:], func=ACT.Tanh)
+                return
+            for k in range(BANKS):
+                nc.scalar.activation(out=pre[k][:], in_=pre[k][:], func=ACT.Sigmoid)
+            if gate == "i":
+                for k in range(BANKS):
+                    nc.vector.tensor_tensor(
+                        out=cell[:, rows_of[k], cols], in0=pre[k][:], in1=cell[:, rows_of[k], cols], op=ALU.mult
+                    )
+                return
+            for k in range(BANKS):
+                nc.vector.tensor_tensor(out=pre[k][:], in0=pre[k][:], in1=c_sb[:, rows_of[k], cols], op=ALU.mult)
+            for k in range(BANKS):
+                nc.vector.tensor_tensor(out=pre[k][:], in0=pre[k][:], in1=cell[:, rows_of[k], cols], op=ALU.add)
+                nc.sync.dma_start(out=out_rows[:, rows_of[k], cols], in_=pre[k][:])
+
+        h_codes, h_scales = quantise_activation("h", h_sb)
+        for chunk in range(CHUNKS):
+            gate_chunk("g", xz_g_sb, bias_g, [(h_codes, h_scales, raw_hg)], chunk)
+        c_codes, c_scales = quantise_activation("c", c_sb)
+        for chunk in range(CHUNKS):
+            gate_chunk(
+                "i", xz_i_sb, bias_i, [(h_codes, h_scales, raw_hi), (c_codes, c_scales, raw_ci)], chunk
+            )
+        for chunk in range(CHUNKS):
+            gate_chunk(
+                "f", xz_f_sb, bias_f, [(h_codes, h_scales, raw_hf), (c_codes, c_scales, raw_cf)], chunk
+            )

@@ -17,13 +17,18 @@ K_PASS = P * PACK
 B = 512
 H = 1024
 M_TILES = B // P
+N_TILES = H // P
 PASSES = H // K_PASS
 BANK = 512
 CH = 256
 CHUNKS = H // CH
+N_PER_CHUNK = CH // P
 M_PER_BANK = BANK // CH
 BANKS = M_TILES // M_PER_BANK
 HALF = H // 2
+SCALAR_TAKES_EVERY = 3
+
+GATE_NUMBER = {"g": 0, "i": 1, "f": 2}
 
 FLOPS = 2 * B * H * H * 5
 
@@ -35,16 +40,20 @@ def tile_residuallstmcell_pa_kernel(
     with ExitStack() as stack:
         keep = stack.enter_context(tc.tile_pool(name="keep", bufs=1))
         regroup = stack.enter_context(tc.tile_pool(name="regroup", bufs=6))
-        quantised = stack.enter_context(tc.tile_pool(name="quantised", bufs=8))
-        work = stack.enter_context(tc.tile_pool(name="work", bufs=14))
-        psum_turn = stack.enter_context(tc.psum_pool(name="psum_turn", bufs=2))
-        psum_acc = stack.enter_context(tc.psum_pool(name="psum_acc", bufs=6))
+        quantised = stack.enter_context(tc.tile_pool(name="quantised", bufs=6))
+        work = stack.enter_context(tc.tile_pool(name="work", bufs=6))
+        psum_t = stack.enter_context(tc.psum_pool(name="psum_t", bufs=4))
+        psum_pre = stack.enter_context(tc.psum_pool(name="psum_pre", bufs=4))
 
-        ident = keep.tile([P, P], F32, name="ident")
-        make_identity(nc, ident[:])
+        ident_f32 = keep.tile([P, P], F32, name="ident_f32")
+        make_identity(nc, ident_f32[:])
+        ident_bf16 = keep.tile([P, P], BF16, name="ident_bf16")
+        make_identity(nc, ident_bf16[:])
         warm = keep.tile([P, 1], F32, name="warm")
         nc.vector.memset(warm[:], 0.0)
         nc.scalar.activation(out=warm[:], in_=warm[:], func=ACT.Sigmoid)
+        bias_rows = keep.tile([P, P], BF16, name="bias_rows")
+        nc.vector.memset(bias_rows[:], 0.0)
 
         def load_rows(name, src):
             rows = keep.tile([P, M_TILES, H], BF16, name=name)
@@ -59,11 +68,6 @@ def tile_residuallstmcell_pa_kernel(
                     in_=w[g * K_PASS : (g + 1) * K_PASS, cols].rearrange("(p j) n -> p j n", j=PACK),
                 )
 
-        def load_bias(name, b):
-            spread = keep.tile([P, H], BF16, name=name)
-            nc.sync.dma_start(out=spread[:], in_=b.partition_broadcast(P))
-            return spread
-
         raw_hg = keep.tile([P, PASSES, PACK, H], BF16, name="raw_hg")
         raw_hi = keep.tile([P, PASSES, PACK, H], BF16, name="raw_hi")
         raw_ci = keep.tile([P, PASSES, PACK, H], BF16, name="raw_ci")
@@ -72,52 +76,56 @@ def tile_residuallstmcell_pa_kernel(
 
         load_weight_half(raw_hg, w_hg, 0)
         h_sb = load_rows("h_sb", h_prev)
+        for q, b in enumerate((b_g, b_i, b_f)):
+            nc.sync.dma_start(
+                out=bias_rows[q * N_TILES : (q + 1) * N_TILES, :], in_=b.rearrange("(j p) -> j p", p=P)
+            )
         load_weight_half(raw_hg, w_hg, 1)
-        bias_g = load_bias("bias_g", b_g)
         xz_g_sb = load_rows("xz_g_sb", xz_g)
         c_sb = load_rows("c_sb", c_prev)
         load_weight_half(raw_hi, w_hi, 0)
         load_weight_half(raw_ci, w_ci, 0)
-        bias_i = load_bias("bias_i", b_i)
         xz_i_sb = load_rows("xz_i_sb", xz_i)
         load_weight_half(raw_hi, w_hi, 1)
         load_weight_half(raw_ci, w_ci, 1)
         load_weight_half(raw_hf, w_hf, 0)
         load_weight_half(raw_cf, w_cf, 0)
-        bias_f = load_bias("bias_f", b_f)
         xz_f_sb = load_rows("xz_f_sb", xz_f)
         load_weight_half(raw_hf, w_hf, 1)
         load_weight_half(raw_cf, w_cf, 1)
 
         def quantise_activation(name, x_sb):
-            codes = keep.tile([P, M_TILES * PASSES * P], U32, name=name + "_codes", align_bytes=64)
-            scales = keep.tile([P, M_TILES * PASSES * P], U8, name=name + "_scales", align_bytes=64)
+            x_grouped = regroup.tile([P, PASSES, B, PACK], BF16, name="x_grouped", bufs=1, align_bytes=64)
             for m in range(M_TILES):
                 words = x_sb[:, m, :].bitcast(F32).rearrange("p (g q u) -> p g u q", g=PASSES, u=2)
-                turned = psum_turn.tile([P, PASSES, 2, P], F32, name="turned")
+                turned = psum_t.tile([P, PASSES, 2, P], F32, name="turned", tag="t")
                 for g in range(PASSES):
                     for u in range(2):
-                        nc.tensor.transpose(turned[:, g, u, :], words[:, g, u, :], ident[:])
-                x_grouped = regroup.tile(
-                    [P, PASSES, P, PACK], BF16, name="x_grouped", bufs=2, align_bytes=64
-                )
+                        nc.tensor.transpose(turned[:, g, u, :], words[:, g, u, :], ident_f32[:])
                 nc.vector.tensor_copy(
-                    out=x_grouped[:].bitcast(F32), in_=turned[:].rearrange("p g u b -> p g b u")
+                    out=x_grouped[:, :, m * P : (m + 1) * P, :].bitcast(F32),
+                    in_=turned[:].rearrange("p g u b -> p g b u"),
                 )
-                span = slice(m * PASSES * P, (m + 1) * PASSES * P)
+            codes = keep.tile([P, PASSES * B], U32, name=name + "_codes", align_bytes=64)
+            scales = keep.tile([P, PASSES * B], U8, name=name + "_scales", align_bytes=64)
+            for g in range(PASSES):
                 nc.vector.quantize_mx(
-                    out=codes[:, span].bitcast(FP8X4),
-                    scales=scales[:, span],
-                    in_=x_grouped[:].rearrange("p g b t -> p (g b t)"),
+                    out=codes[:, g * B : (g + 1) * B].bitcast(FP8X4),
+                    scales=scales[:, g * B : (g + 1) * B],
+                    in_=x_grouped[:, g].rearrange("p b t -> p (b t)"),
                 )
             return codes, scales
 
-        def quantise_weight_chunk(raw, chunk):
+        def quantise_weight_chunk(raw, weight_index, chunk):
             w_grouped = regroup.tile([P, PASSES, CH, PACK], BF16, name="w_grouped", align_bytes=64)
             for g in range(PASSES):
                 src = raw[:, g, :, chunk * CH : (chunk + 1) * CH].rearrange("p t (c i) -> p c t i", i=4)
                 dst = w_grouped[:, g].rearrange("p (c i) t -> p c t i", i=4)
-                nc.scalar.copy(out=dst, in_=src)
+                piece = (weight_index * CHUNKS + chunk) * PASSES + g
+                if piece % SCALAR_TAKES_EVERY == SCALAR_TAKES_EVERY - 1:
+                    nc.scalar.copy(out=dst, in_=src)
+                else:
+                    nc.vector.tensor_copy(out=dst, in_=src)
             w_codes = quantised.tile([P, PASSES * CH], U32, name="w_codes", align_bytes=64)
             w_scales = quantised.tile([P, PASSES * CH], U8, name="w_scales", align_bytes=64)
             nc.vector.quantize_mx(
@@ -130,71 +138,88 @@ def tile_residuallstmcell_pa_kernel(
         cell = keep.tile([P, M_TILES, H], F32, name="cell")
         out_rows = out.rearrange("(m p) n -> p m n", p=P)
 
-        def gate_chunk(gate, xz_sb, bias, products, chunk):
+        def gate_chunk(gate, xz_sb, products, chunk):
             cols = slice(chunk * CH, (chunk + 1) * CH)
             operands = []
-            for x_codes, x_scales, raw in products:
-                w_codes, w_scales = quantise_weight_chunk(raw, chunk)
+            for x_codes, x_scales, raw, weight_index in products:
+                w_codes, w_scales = quantise_weight_chunk(raw, weight_index, chunk)
                 for g in range(PASSES):
                     operands.append((x_codes, x_scales, w_codes, w_scales, g))
 
-            rows_of = [slice(k * M_PER_BANK, (k + 1) * M_PER_BANK) for k in range(BANKS)]
-            pre = []
-            for k in range(BANKS):
-                pre_k = work.tile([P, M_PER_BANK, CH], F32, name="pre")
-                nc.vector.tensor_tensor(
-                    out=pre_k[:],
-                    in0=xz_sb[:, rows_of[k], cols],
-                    in1=bias[:, cols].unsqueeze(1).to_broadcast([P, M_PER_BANK, CH]),
-                    op=ALU.add,
+            biased = []
+            for j in range(N_PER_CHUNK):
+                sums_t = psum_t.tile([P, B], F32, name="sums_t", tag="t")
+                for step, (x_codes, x_scales, w_codes, w_scales, g) in enumerate(operands):
+                    w_cols = slice(g * CH + j * P, g * CH + (j + 1) * P)
+                    x_cols = slice(g * B, (g + 1) * B)
+                    nc.tensor.matmul_mx(
+                        out=sums_t[:],
+                        lhsT=w_codes[:, w_cols].bitcast(FP8X4),
+                        lhsT_scale=w_scales[:, w_cols],
+                        rhs=x_codes[:, x_cols].bitcast(FP8X4),
+                        rhs_scale=x_scales[:, x_cols],
+                        start=(step == 0),
+                        stop=(step == len(operands) - 1),
+                    )
+                biased_j = work.tile([P, B], F32, name="biased")
+                column = GATE_NUMBER[gate] * N_TILES + chunk * N_PER_CHUNK + j
+                nc.scalar.activation(
+                    out=biased_j[:], in_=sums_t[:], func=ACT.Identity, bias=bias_cols[:, column : column + 1]
                 )
-                pre.append(pre_k)
+                biased.append(biased_j)
 
+            rows_of = [slice(k * M_PER_BANK, (k + 1) * M_PER_BANK) for k in range(BANKS)]
+            gated = []
             for k in range(BANKS):
-                acc = psum_acc.tile([P, M_PER_BANK, CH], F32, name="acc")
+                pre = psum_pre.tile([P, M_PER_BANK, CH], F32, name="pre")
                 for s in range(M_PER_BANK):
                     m = k * M_PER_BANK + s
-                    for step, (x_codes, x_scales, w_codes, w_scales, g) in enumerate(operands):
-                        x_cols = slice((m * PASSES + g) * P, (m * PASSES + g + 1) * P)
-                        w_cols = slice(g * CH, (g + 1) * CH)
-                        nc.tensor.matmul_mx(
-                            out=acc[:, s, :],
-                            lhsT=x_codes[:, x_cols].bitcast(FP8X4),
-                            lhsT_scale=x_scales[:, x_cols],
-                            rhs=w_codes[:, w_cols].bitcast(FP8X4),
-                            rhs_scale=w_scales[:, w_cols],
-                            start=(step == 0),
-                            stop=(step == len(operands) - 1),
+                    for j in range(N_PER_CHUNK):
+                        nc.tensor.matmul(
+                            out=pre[:, s, j * P : (j + 1) * P],
+                            lhsT=biased[j][:, m * P : (m + 1) * P],
+                            rhs=ident_f32[:],
+                            is_transpose=True,
+                            start=(j == 0),
+                            stop=False,
                         )
-                nc.vector.tensor_tensor(out=pre[k][:], in0=acc[:], in1=pre[k][:], op=ALU.add)
+                    nc.tensor.matmul(
+                        out=pre[:, s, :], lhsT=ident_bf16[:], rhs=xz_sb[:, m, cols], start=False, stop=True
+                    )
+                if gate == "g":
+                    nc.scalar.activation(out=cell[:, rows_of[k], cols], in_=pre[:], func=ACT.Tanh)
+                else:
+                    gated_k = work.tile([P, M_PER_BANK, CH], F32, name="gated")
+                    nc.scalar.activation(out=gated_k[:], in_=pre[:], func=ACT.Sigmoid)
+                    gated.append(gated_k)
 
-            if gate == "g":
-                for k in range(BANKS):
-                    nc.scalar.activation(out=cell[:, rows_of[k], cols], in_=pre[k][:], func=ACT.Tanh)
-                return
-            for k in range(BANKS):
-                nc.scalar.activation(out=pre[k][:], in_=pre[k][:], func=ACT.Sigmoid)
             if gate == "i":
                 for k in range(BANKS):
                     nc.vector.tensor_tensor(
-                        out=cell[:, rows_of[k], cols], in0=pre[k][:], in1=cell[:, rows_of[k], cols], op=ALU.mult
+                        out=cell[:, rows_of[k], cols], in0=gated[k][:], in1=cell[:, rows_of[k], cols], op=ALU.mult
                     )
-                return
-            for k in range(BANKS):
-                nc.vector.tensor_tensor(out=pre[k][:], in0=pre[k][:], in1=c_sb[:, rows_of[k], cols], op=ALU.mult)
-            for k in range(BANKS):
-                nc.vector.tensor_tensor(out=pre[k][:], in0=pre[k][:], in1=cell[:, rows_of[k], cols], op=ALU.add)
-                nc.sync.dma_start(out=out_rows[:, rows_of[k], cols], in_=pre[k][:])
+            if gate == "f":
+                for k in range(BANKS):
+                    nc.vector.tensor_tensor(
+                        out=gated[k][:], in0=gated[k][:], in1=c_sb[:, rows_of[k], cols], op=ALU.mult
+                    )
+                for k in range(BANKS):
+                    nc.vector.tensor_tensor(
+                        out=gated[k][:], in0=gated[k][:], in1=cell[:, rows_of[k], cols], op=ALU.add
+                    )
+                    nc.sync.dma_start(out=out_rows[:, rows_of[k], cols], in_=gated[k][:])
 
         h_codes, h_scales = quantise_activation("h", h_sb)
+
+        bias_t = psum_t.tile([P, P], BF16, name="bias_t", tag="t")
+        nc.tensor.transpose(bias_t[:], bias_rows[:], ident_bf16[:])
+        bias_cols = keep.tile([P, 3 * N_TILES], F32, name="bias_cols")
+        nc.vector.tensor_copy(out=bias_cols[:], in_=bias_t[:, 0 : 3 * N_TILES])
+
         for chunk in range(CHUNKS):
-            gate_chunk("g", xz_g_sb, bias_g, [(h_codes, h_scales, raw_hg)], chunk)
+            gate_chunk("g", xz_g_sb, [(h_codes, h_scales, raw_hg, 0)], chunk)
         c_codes, c_scales = quantise_activation("c", c_sb)
         for chunk in range(CHUNKS):
-            gate_chunk(
-                "i", xz_i_sb, bias_i, [(h_codes, h_scales, raw_hi), (c_codes, c_scales, raw_ci)], chunk
-            )
+            gate_chunk("i", xz_i_sb, [(h_codes, h_scales, raw_hi, 1), (c_codes, c_scales, raw_ci, 2)], chunk)
         for chunk in range(CHUNKS):
-            gate_chunk(
-                "f", xz_f_sb, bias_f, [(h_codes, h_scales, raw_hf), (c_codes, c_scales, raw_cf)], chunk
-            )
+            gate_chunk("f", xz_f_sb, [(h_codes, h_scales, raw_hf, 3), (c_codes, c_scales, raw_cf, 4)], chunk)

@@ -26,9 +26,7 @@ N_PER_CHUNK = CH // P
 M_PER_BANK = BANK // CH
 BANKS = M_TILES // M_PER_BANK
 HALF = H // 2
-SCALAR_TAKES_EVERY = 3
-
-GATE_NUMBER = {"g": 0, "i": 1, "f": 2}
+GATES = ("g", "i", "f")
 
 FLOPS = 2 * B * H * H * 5
 
@@ -39,11 +37,13 @@ def tile_residuallstmcell_pa_kernel(
     nc = tc.nc
     with ExitStack() as stack:
         keep = stack.enter_context(tc.tile_pool(name="keep", bufs=1))
-        regroup = stack.enter_context(tc.tile_pool(name="regroup", bufs=6))
+        regroup = stack.enter_context(tc.tile_pool(name="regroup", bufs=8))
         quantised = stack.enter_context(tc.tile_pool(name="quantised", bufs=6))
         work = stack.enter_context(tc.tile_pool(name="work", bufs=6))
-        psum_t = stack.enter_context(tc.psum_pool(name="psum_t", bufs=4))
-        psum_pre = stack.enter_context(tc.psum_pool(name="psum_pre", bufs=4))
+        psum_turn = stack.enter_context(tc.psum_pool(name="psum_turn", bufs=2))
+        psum_sums = stack.enter_context(tc.psum_pool(name="psum_sums", bufs=4))
+        psum_pre = stack.enter_context(tc.psum_pool(name="psum_pre", bufs=2))
+        stack.enter_context(tc.manual_schedule())
 
         ident_f32 = keep.tile([P, P], F32, name="ident_f32")
         make_identity(nc, ident_f32[:])
@@ -74,8 +74,8 @@ def tile_residuallstmcell_pa_kernel(
         raw_hf = keep.tile([P, PASSES, PACK, H], BF16, name="raw_hf")
         raw_cf = keep.tile([P, PASSES, PACK, H], BF16, name="raw_cf")
 
-        load_weight_half(raw_hg, w_hg, 0)
         h_sb = load_rows("h_sb", h_prev)
+        load_weight_half(raw_hg, w_hg, 0)
         for q, b in enumerate((b_g, b_i, b_f)):
             nc.sync.dma_start(
                 out=bias_rows[q * N_TILES : (q + 1) * N_TILES, :], in_=b.rearrange("(j p) -> j p", p=P)
@@ -85,20 +85,31 @@ def tile_residuallstmcell_pa_kernel(
         c_sb = load_rows("c_sb", c_prev)
         load_weight_half(raw_hi, w_hi, 0)
         load_weight_half(raw_ci, w_ci, 0)
-        xz_i_sb = load_rows("xz_i_sb", xz_i)
         load_weight_half(raw_hi, w_hi, 1)
         load_weight_half(raw_ci, w_ci, 1)
+        xz_i_sb = load_rows("xz_i_sb", xz_i)
         load_weight_half(raw_hf, w_hf, 0)
         load_weight_half(raw_cf, w_cf, 0)
-        xz_f_sb = load_rows("xz_f_sb", xz_f)
         load_weight_half(raw_hf, w_hf, 1)
         load_weight_half(raw_cf, w_cf, 1)
+        xz_f_sb = load_rows("xz_f_sb", xz_f)
 
-        def quantise_activation(name, x_sb):
+        rows_in_sbuf = {"h": h_sb, "c": c_sb}
+        xz_of = {"g": xz_g_sb, "i": xz_i_sb, "f": xz_f_sb}
+        products_of = {
+            "g": [("h", raw_hg)],
+            "i": [("h", raw_hi), ("c", raw_ci)],
+            "f": [("h", raw_hf), ("c", raw_cf)],
+        }
+
+        x_quantised = {}
+
+        def quantise_activation(name):
+            x_sb = rows_in_sbuf[name]
             x_grouped = regroup.tile([P, PASSES, B, PACK], BF16, name="x_grouped", bufs=1, align_bytes=64)
             for m in range(M_TILES):
                 words = x_sb[:, m, :].bitcast(F32).rearrange("p (g q u) -> p g u q", g=PASSES, u=2)
-                turned = psum_t.tile([P, PASSES, 2, P], F32, name="turned", tag="t")
+                turned = psum_turn.tile([P, PASSES, 2, P], F32, name="turned")
                 for g in range(PASSES):
                     for u in range(2):
                         nc.tensor.transpose(turned[:, g, u, :], words[:, g, u, :], ident_f32[:])
@@ -114,41 +125,58 @@ def tile_residuallstmcell_pa_kernel(
                     scales=scales[:, g * B : (g + 1) * B],
                     in_=x_grouped[:, g].rearrange("p b t -> p (b t)"),
                 )
-            return codes, scales
+            x_quantised[name] = (codes, scales)
 
-        def quantise_weight_chunk(raw, weight_index, chunk):
-            w_grouped = regroup.tile([P, PASSES, CH, PACK], BF16, name="w_grouped", align_bytes=64)
-            for g in range(PASSES):
-                src = raw[:, g, :, chunk * CH : (chunk + 1) * CH].rearrange("p t (c i) -> p c t i", i=4)
-                dst = w_grouped[:, g].rearrange("p (c i) t -> p c t i", i=4)
-                piece = (weight_index * CHUNKS + chunk) * PASSES + g
-                if piece % SCALAR_TAKES_EVERY == SCALAR_TAKES_EVERY - 1:
-                    nc.scalar.copy(out=dst, in_=src)
-                else:
-                    nc.vector.tensor_copy(out=dst, in_=src)
-            w_codes = quantised.tile([P, PASSES * CH], U32, name="w_codes", align_bytes=64)
-            w_scales = quantised.tile([P, PASSES * CH], U8, name="w_scales", align_bytes=64)
-            nc.vector.quantize_mx(
-                out=w_codes[:].bitcast(FP8X4),
-                scales=w_scales[:],
-                in_=w_grouped[:].rearrange("p g c t -> p (g c t)"),
-            )
-            return w_codes, w_scales
-
+        units = [(gate, chunk) for gate in GATES for chunk in range(CHUNKS)]
+        w_grouped_of = {}
+        w_quantised_of = {}
+        sums_of = {}
+        biased_of = {}
+        pre_of = {}
+        gated_of = {}
+        rows_of = [slice(k * M_PER_BANK, (k + 1) * M_PER_BANK) for k in range(BANKS)]
         cell = keep.tile([P, M_TILES, H], F32, name="cell")
         out_rows = out.rearrange("(m p) n -> p m n", p=P)
 
-        def gate_chunk(gate, xz_sb, products, chunk):
-            cols = slice(chunk * CH, (chunk + 1) * CH)
+        def regroup_weights(u, engine):
+            gate, chunk = units[u]
+            if u not in w_grouped_of:
+                w_grouped_of[u] = [
+                    regroup.tile([P, PASSES, CH, PACK], BF16, name="w_grouped", align_bytes=64)
+                    for product in products_of[gate]
+                ]
+            last_piece = len(products_of[gate]) * PASSES - 1
+            for w, (x_name, raw) in enumerate(products_of[gate]):
+                for g in range(PASSES):
+                    src = raw[:, g, :, chunk * CH : (chunk + 1) * CH].rearrange("p t (c i) -> p c t i", i=4)
+                    dst = w_grouped_of[u][w][:, g].rearrange("p (c i) t -> p c t i", i=4)
+                    if w * PASSES + g == last_piece and engine == "scalar":
+                        nc.scalar.copy(out=dst, in_=src)
+                    if w * PASSES + g != last_piece and engine == "vector":
+                        nc.vector.tensor_copy(out=dst, in_=src)
+
+        def quantise_weights(u):
+            w_quantised_of[u] = []
+            for w_grouped in w_grouped_of[u]:
+                w_codes = quantised.tile([P, PASSES * CH], U32, name="w_codes", align_bytes=64)
+                w_scales = quantised.tile([P, PASSES * CH], U8, name="w_scales", align_bytes=64)
+                nc.vector.quantize_mx(
+                    out=w_codes[:].bitcast(FP8X4),
+                    scales=w_scales[:],
+                    in_=w_grouped[:].rearrange("p g c t -> p (g c t)"),
+                )
+                w_quantised_of[u].append((w_codes, w_scales))
+
+        def multiply(u):
+            gate, chunk = units[u]
             operands = []
-            for x_codes, x_scales, raw, weight_index in products:
-                w_codes, w_scales = quantise_weight_chunk(raw, weight_index, chunk)
+            for (x_name, raw), (w_codes, w_scales) in zip(products_of[gate], w_quantised_of[u]):
+                x_codes, x_scales = x_quantised[x_name]
                 for g in range(PASSES):
                     operands.append((x_codes, x_scales, w_codes, w_scales, g))
-
-            biased = []
+            sums_of[u] = []
             for j in range(N_PER_CHUNK):
-                sums_t = psum_t.tile([P, B], F32, name="sums_t", tag="t")
+                sums_t = psum_sums.tile([P, B], F32, name="sums_t")
                 for step, (x_codes, x_scales, w_codes, w_scales, g) in enumerate(operands):
                     w_cols = slice(g * CH + j * P, g * CH + (j + 1) * P)
                     x_cols = slice(g * B, (g + 1) * B)
@@ -161,65 +189,93 @@ def tile_residuallstmcell_pa_kernel(
                         start=(step == 0),
                         stop=(step == len(operands) - 1),
                     )
-                biased_j = work.tile([P, B], F32, name="biased")
-                column = GATE_NUMBER[gate] * N_TILES + chunk * N_PER_CHUNK + j
-                nc.scalar.activation(
-                    out=biased_j[:], in_=sums_t[:], func=ACT.Identity, bias=bias_cols[:, column : column + 1]
-                )
-                biased.append(biased_j)
+                sums_of[u].append(sums_t)
 
-            rows_of = [slice(k * M_PER_BANK, (k + 1) * M_PER_BANK) for k in range(BANKS)]
-            gated = []
+        def add_bias(u):
+            gate, chunk = units[u]
+            biased_of[u] = []
+            for j, sums_t in enumerate(sums_of[u]):
+                biased = work.tile([P, B], F32, name="biased")
+                column = GATES.index(gate) * N_TILES + chunk * N_PER_CHUNK + j
+                nc.scalar.activation(
+                    out=biased[:], in_=sums_t[:], func=ACT.Identity, bias=bias_cols[:, column : column + 1]
+                )
+                biased_of[u].append(biased)
+
+        def turn_back_and_add_xz(u):
+            gate, chunk = units[u]
+            pre_of[u] = []
             for k in range(BANKS):
                 pre = psum_pre.tile([P, M_PER_BANK, CH], F32, name="pre")
                 for s in range(M_PER_BANK):
                     m = k * M_PER_BANK + s
-                    for j in range(N_PER_CHUNK):
+                    for j, biased in enumerate(biased_of[u]):
                         nc.tensor.matmul(
                             out=pre[:, s, j * P : (j + 1) * P],
-                            lhsT=biased[j][:, m * P : (m + 1) * P],
+                            lhsT=biased[:, m * P : (m + 1) * P],
                             rhs=ident_f32[:],
                             is_transpose=True,
                             start=(j == 0),
                             stop=False,
                         )
                     nc.tensor.matmul(
-                        out=pre[:, s, :], lhsT=ident_bf16[:], rhs=xz_sb[:, m, cols], start=False, stop=True
+                        out=pre[:, s, :],
+                        lhsT=ident_bf16[:],
+                        rhs=xz_of[gate][:, m, chunk * CH : (chunk + 1) * CH],
+                        start=False,
+                        stop=True,
                     )
+                pre_of[u].append(pre)
+
+        def activate(u):
+            gate, chunk = units[u]
+            cols = slice(chunk * CH, (chunk + 1) * CH)
+            gated_of[u] = []
+            for k, pre in enumerate(pre_of[u]):
                 if gate == "g":
                     nc.scalar.activation(out=cell[:, rows_of[k], cols], in_=pre[:], func=ACT.Tanh)
                 else:
-                    gated_k = work.tile([P, M_PER_BANK, CH], F32, name="gated")
-                    nc.scalar.activation(out=gated_k[:], in_=pre[:], func=ACT.Sigmoid)
-                    gated.append(gated_k)
+                    gated = work.tile([P, M_PER_BANK, CH], F32, name="gated")
+                    nc.scalar.activation(out=gated[:], in_=pre[:], func=ACT.Sigmoid)
+                    gated_of[u].append(gated)
 
+        def combine(u):
+            gate, chunk = units[u]
+            cols = slice(chunk * CH, (chunk + 1) * CH)
             if gate == "i":
-                for k in range(BANKS):
+                for k, gated in enumerate(gated_of[u]):
                     nc.vector.tensor_tensor(
-                        out=cell[:, rows_of[k], cols], in0=gated[k][:], in1=cell[:, rows_of[k], cols], op=ALU.mult
+                        out=cell[:, rows_of[k], cols], in0=gated[:], in1=cell[:, rows_of[k], cols], op=ALU.mult
                     )
             if gate == "f":
-                for k in range(BANKS):
-                    nc.vector.tensor_tensor(
-                        out=gated[k][:], in0=gated[k][:], in1=c_sb[:, rows_of[k], cols], op=ALU.mult
-                    )
-                for k in range(BANKS):
-                    nc.vector.tensor_tensor(
-                        out=gated[k][:], in0=gated[k][:], in1=cell[:, rows_of[k], cols], op=ALU.add
-                    )
-                    nc.sync.dma_start(out=out_rows[:, rows_of[k], cols], in_=gated[k][:])
+                for k, gated in enumerate(gated_of[u]):
+                    nc.vector.tensor_tensor(out=gated[:], in0=gated[:], in1=c_sb[:, rows_of[k], cols], op=ALU.mult)
+                for k, gated in enumerate(gated_of[u]):
+                    nc.vector.tensor_tensor(out=gated[:], in0=gated[:], in1=cell[:, rows_of[k], cols], op=ALU.add)
+                    nc.sync.dma_start(out=out_rows[:, rows_of[k], cols], in_=gated[:])
 
-        h_codes, h_scales = quantise_activation("h", h_sb)
+        def make_ready(u):
+            for x_name, raw in products_of[units[u][0]]:
+                if x_name not in x_quantised:
+                    quantise_activation(x_name)
 
-        bias_t = psum_t.tile([P, P], BF16, name="bias_t", tag="t")
+        def run(stage, u, *more):
+            if 0 <= u < len(units):
+                stage(u, *more)
+
+        make_ready(0)
+        bias_t = psum_turn.tile([P, P], BF16, name="bias_t", tag="turned")
         nc.tensor.transpose(bias_t[:], bias_rows[:], ident_bf16[:])
-        bias_cols = keep.tile([P, 3 * N_TILES], F32, name="bias_cols")
-        nc.vector.tensor_copy(out=bias_cols[:], in_=bias_t[:, 0 : 3 * N_TILES])
+        bias_cols = keep.tile([P, len(GATES) * N_TILES], F32, name="bias_cols")
+        nc.vector.tensor_copy(out=bias_cols[:], in_=bias_t[:, 0 : len(GATES) * N_TILES])
 
-        for chunk in range(CHUNKS):
-            gate_chunk("g", xz_g_sb, [(h_codes, h_scales, raw_hg, 0)], chunk)
-        c_codes, c_scales = quantise_activation("c", c_sb)
-        for chunk in range(CHUNKS):
-            gate_chunk("i", xz_i_sb, [(h_codes, h_scales, raw_hi, 1), (c_codes, c_scales, raw_ci, 2)], chunk)
-        for chunk in range(CHUNKS):
-            gate_chunk("f", xz_f_sb, [(h_codes, h_scales, raw_hf, 3), (c_codes, c_scales, raw_cf, 4)], chunk)
+        for step in range(len(units) + 4):
+            run(regroup_weights, step, "scalar")
+            run(quantise_weights, step - 1)
+            run(add_bias, step - 2)
+            run(turn_back_and_add_xz, step - 3)
+            run(multiply, step - 1)
+            run(activate, step - 3)
+            run(regroup_weights, step, "vector")
+            run(combine, step - 4)
+            run(make_ready, step + 1)

@@ -43,7 +43,6 @@ def tile_residuallstmcell_pa_kernel(
         psum_turn = stack.enter_context(tc.psum_pool(name="psum_turn", bufs=2))
         psum_sums = stack.enter_context(tc.psum_pool(name="psum_sums", bufs=4))
         psum_pre = stack.enter_context(tc.psum_pool(name="psum_pre", bufs=2))
-        stack.enter_context(tc.manual_schedule())
 
         ident_f32 = keep.tile([P, P], F32, name="ident_f32")
         make_identity(nc, ident_f32[:])
@@ -57,7 +56,7 @@ def tile_residuallstmcell_pa_kernel(
 
         def load_rows(name, src):
             rows = keep.tile([P, M_TILES, H], BF16, name=name)
-            nc.sync.dma_start(out=rows[:], in_=src.rearrange("(m p) n -> p m n", p=P))
+            nc.sync.dma_start(out=rows[:], in_=src.rearrange("(p m) n -> p m n", m=M_TILES))
             return rows
 
         def load_weight_half(raw, w, half):
@@ -113,7 +112,7 @@ def tile_residuallstmcell_pa_kernel(
                 for g in range(PASSES):
                     for u in range(2):
                         nc.tensor.transpose(turned[:, g, u, :], words[:, g, u, :], ident_f32[:])
-                nc.vector.tensor_copy(
+                nc.scalar.copy(
                     out=x_grouped[:, :, m * P : (m + 1) * P, :].bitcast(F32),
                     in_=turned[:].rearrange("p g u b -> p g b u"),
                 )
@@ -136,7 +135,7 @@ def tile_residuallstmcell_pa_kernel(
         gated_of = {}
         rows_of = [slice(k * M_PER_BANK, (k + 1) * M_PER_BANK) for k in range(BANKS)]
         cell = keep.tile([P, M_TILES, H], F32, name="cell")
-        out_rows = out.rearrange("(m p) n -> p m n", p=P)
+        out_rows = out.rearrange("(p m) n -> p m n", m=M_TILES)
 
         def regroup_weights(u, engine):
             gate, chunk = units[u]

@@ -10,7 +10,6 @@ U8 = mybir.dt.uint8
 FP8X4 = mybir.dt.float8_e4m3fn_x4
 ACT = mybir.ActivationFunctionType
 ALU = mybir.AluOpType
-
 P = 128
 PACK = 4
 K_PASS = P * PACK
@@ -19,16 +18,19 @@ H = 1024
 M_TILES = B // P
 N_TILES = H // P
 PASSES = H // K_PASS
-BANK = 512
-CH = 256
-CHUNKS = H // CH
-N_PER_CHUNK = CH // P
-M_PER_BANK = BANK // CH
-BANKS = M_TILES // M_PER_BANK
 HALF = H // 2
-GATES = ("g", "i", "f")
-
 FLOPS = 2 * B * H * H * 5
+
+GATES = ("g", "i", "f")
+LOADS = "hg0a h hg1a bias hg0b hg1b hi0a xg hi1a c ci0a ci1a hi0b hi1b ci0b ci1b xi hf0 hf1 cf0 cf1 xf".split()
+SV = {"hg": 384, "hg0a": 256, "hi": 416, "ci": 416, "hf": 352, "cf": 384}
+NSUM, NPRE, NTURN, WG, WQ, WKB, WKG = 4, 2, 2, 4, 5, 4, 4
+A_LAG = 2
+T_LAG = 2
+K_LAG = 3
+V_ORDER = "hg0a qhg0a hg1a hg0b qh qhg1a hg1b qhg0b hi0a qhg1b hi1a qhi0a qhi1a qc ci0a ci1a qci0a hi0b qci1a hi1b qhi0b ci0b qhi1b ci1b qci0b hf0a qci1b hf1a qhf0a K8 qhf1a cf0a K9 cf1a qcf0a hf0b qcf1a hf1b qhf0b K10 qhf1b cf0b K11 cf1b qcf0b K12 qcf1b K13 K14 K15 K16 K17 K18 K19 K20 K21 K22 K23".split()
+S_ORDER = "hg0a xh hg1a bias hg0b hg1b B0 B1 hi0a B2 B3 A0 A1 hi1a xc B4 B5 A2 A3 ci0a ci1a B6 B7 A4 A5 hi0b hi1b A6 A7 B8 B9 ci0b ci1b B10 B11 A8 A9 hf0a hf1a B12 B13 A10 A11 cf0a cf1a B14 B15 A12 A13 hf0b hf1b A14 A15 B16 B17 cf0b cf1b B18 B19 A16 A17 B20 B21 A18 A19 B22 B23 A20 A21 A22 A23".split()
+PE_ORDER = "xh bias M0 M1 M2 M3 T0 T1 xc M4 M5 T2 T3 M6 M7 T4 T5 T6 T7 M8 M9 M10 M11 T8 T9 M12 M13 T10 T11 M14 M15 T12 T13 T14 T15 M16 M17 M18 M19 T16 T17 M20 M21 T18 T19 M22 M23 T20 T21 T22 T23".split()
 
 
 def tile_residuallstmcell_pa_kernel(
@@ -37,244 +39,268 @@ def tile_residuallstmcell_pa_kernel(
     nc = tc.nc
     with ExitStack() as stack:
         keep = stack.enter_context(tc.tile_pool(name="keep", bufs=1))
-        regroup = stack.enter_context(tc.tile_pool(name="regroup", bufs=8))
-        quantised = stack.enter_context(tc.tile_pool(name="quantised", bufs=6))
-        work = stack.enter_context(tc.tile_pool(name="work", bufs=6))
-        psum_turn = stack.enter_context(tc.psum_pool(name="psum_turn", bufs=2))
-        psum_sums = stack.enter_context(tc.psum_pool(name="psum_sums", bufs=4))
-        psum_pre = stack.enter_context(tc.psum_pool(name="psum_pre", bufs=2))
+        regroup = stack.enter_context(tc.tile_pool(name="regroup", bufs=WG))
+        quantised = stack.enter_context(tc.tile_pool(name="quantised", bufs=WQ))
+        work = stack.enter_context(tc.tile_pool(name="work", bufs=WKB))
+        psum_turn = stack.enter_context(tc.psum_pool(name="psum_turn", bufs=NTURN))
+        psum_sums = stack.enter_context(tc.psum_pool(name="psum_sums", bufs=NSUM))
+        psum_pre = stack.enter_context(tc.psum_pool(name="psum_pre", bufs=NPRE))
+        stack.enter_context(tc.manual_schedule())
 
-        ident_f32 = keep.tile([P, P], F32, name="ident_f32")
-        make_identity(nc, ident_f32[:])
-        ident_bf16 = keep.tile([P, P], BF16, name="ident_bf16")
-        make_identity(nc, ident_bf16[:])
         warm = keep.tile([P, 1], F32, name="warm")
         nc.vector.memset(warm[:], 0.0)
         nc.scalar.activation(out=warm[:], in_=warm[:], func=ACT.Sigmoid)
         bias_rows = keep.tile([P, P], BF16, name="bias_rows")
         nc.vector.memset(bias_rows[:], 0.0)
+        ident_f32 = keep.tile([P, P], F32, name="ident_f32")
+        make_identity(nc, ident_f32[:])
+        ident_bf16 = keep.tile([P, P], BF16, name="ident_bf16")
+        make_identity(nc, ident_bf16[:])
 
-        def load_rows(name, src):
-            rows = keep.tile([P, M_TILES, H], BF16, name=name)
-            nc.sync.dma_start(out=rows[:], in_=src.rearrange("(p m) n -> p m n", m=M_TILES))
-            return rows
-
-        def load_weight_half(raw, w, half):
-            cols = slice(half * HALF, (half + 1) * HALF)
-            for g in range(PASSES):
+        w_dram = {"hg": w_hg, "hi": w_hi, "ci": w_ci, "hf": w_hf, "cf": w_cf}
+        rows_dram = {"h": h_prev, "c": c_prev, "xg": xz_g, "xi": xz_i, "xf": xz_f}
+        bias_dram = {"g": b_g, "i": b_i, "f": b_f}
+        raw = {}
+        rows = {}
+        for item in LOADS:
+            if item == "bias":
+                for q, gate in enumerate(GATES):
+                    nc.sync.dma_start(
+                        out=bias_rows[q * N_TILES : (q + 1) * N_TILES, :],
+                        in_=bias_dram[gate].rearrange("(j p) -> j p", p=P),
+                    )
+            elif item in rows_dram:
+                rows[item] = keep.tile([P, M_TILES, H], BF16, name=item + "_rows")
+                nc.sync.dma_start(out=rows[item][:], in_=rows_dram[item].rearrange("(p m) n -> p m n", m=M_TILES))
+            else:
+                name, g = item[:2], int(item[2])
+                cols = {"": slice(0, H), "a": slice(0, HALF), "b": slice(HALF, H)}[item[3:]]
+                width = cols.stop - cols.start
+                piece = keep.tile([P, PACK, width], BF16, name="raw_" + item)
                 nc.sync.dma_start(
-                    out=raw[:, g, :, cols],
-                    in_=w[g * K_PASS : (g + 1) * K_PASS, cols].rearrange("(p j) n -> p j n", j=PACK),
+                    out=piece[:],
+                    in_=w_dram[name][g * K_PASS : (g + 1) * K_PASS, cols].rearrange("(p j) n -> p j n", j=PACK),
                 )
+                for half in item[3:] or "ab":
+                    raw[name + item[2] + half] = piece[:, :, 0:HALF] if item[3:] or half == "a" else piece[:, :, HALF:H]
 
-        raw_hg = keep.tile([P, PASSES, PACK, H], BF16, name="raw_hg")
-        raw_hi = keep.tile([P, PASSES, PACK, H], BF16, name="raw_hi")
-        raw_ci = keep.tile([P, PASSES, PACK, H], BF16, name="raw_ci")
-        raw_hf = keep.tile([P, PASSES, PACK, H], BF16, name="raw_hf")
-        raw_cf = keep.tile([P, PASSES, PACK, H], BF16, name="raw_cf")
-
-        h_sb = load_rows("h_sb", h_prev)
-        load_weight_half(raw_hg, w_hg, 0)
-        for q, b in enumerate((b_g, b_i, b_f)):
-            nc.sync.dma_start(
-                out=bias_rows[q * N_TILES : (q + 1) * N_TILES, :], in_=b.rearrange("(j p) -> j p", p=P)
-            )
-        load_weight_half(raw_hg, w_hg, 1)
-        xz_g_sb = load_rows("xz_g_sb", xz_g)
-        c_sb = load_rows("c_sb", c_prev)
-        load_weight_half(raw_hi, w_hi, 0)
-        load_weight_half(raw_ci, w_ci, 0)
-        load_weight_half(raw_hi, w_hi, 1)
-        load_weight_half(raw_ci, w_ci, 1)
-        xz_i_sb = load_rows("xz_i_sb", xz_i)
-        load_weight_half(raw_hf, w_hf, 0)
-        load_weight_half(raw_cf, w_cf, 0)
-        load_weight_half(raw_hf, w_hf, 1)
-        load_weight_half(raw_cf, w_cf, 1)
-        xz_f_sb = load_rows("xz_f_sb", xz_f)
-
-        rows_in_sbuf = {"h": h_sb, "c": c_sb}
-        xz_of = {"g": xz_g_sb, "i": xz_i_sb, "f": xz_f_sb}
-        products_of = {
-            "g": [("h", raw_hg)],
-            "i": [("h", raw_hi), ("c", raw_ci)],
-            "f": [("h", raw_hf), ("c", raw_cf)],
-        }
-
-        x_quantised = {}
-
-        def quantise_activation(name):
-            x_sb = rows_in_sbuf[name]
-            x_grouped = regroup.tile([P, PASSES, B, PACK], BF16, name="x_grouped", bufs=1, align_bytes=64)
-            for m in range(M_TILES):
-                words = x_sb[:, m, :].bitcast(F32).rearrange("p (g q u) -> p g u q", g=PASSES, u=2)
-                turned = psum_turn.tile([P, PASSES, 2, P], F32, name="turned")
-                for g in range(PASSES):
-                    for u in range(2):
-                        nc.tensor.transpose(turned[:, g, u, :], words[:, g, u, :], ident_f32[:])
-                nc.scalar.copy(
-                    out=x_grouped[:, :, m * P : (m + 1) * P, :].bitcast(F32),
-                    in_=turned[:].rearrange("p g u b -> p g b u"),
-                )
-            codes = keep.tile([P, PASSES * B], U32, name=name + "_codes", align_bytes=64)
-            scales = keep.tile([P, PASSES * B], U8, name=name + "_scales", align_bytes=64)
-            for g in range(PASSES):
-                nc.vector.quantize_mx(
-                    out=codes[:, g * B : (g + 1) * B].bitcast(FP8X4),
-                    scales=scales[:, g * B : (g + 1) * B],
-                    in_=x_grouped[:, g].rearrange("p b t -> p (b t)"),
-                )
-            x_quantised[name] = (codes, scales)
-
-        units = [(gate, chunk) for gate in GATES for chunk in range(CHUNKS)]
-        w_grouped_of = {}
-        w_quantised_of = {}
+        products_of = {"g": ["hg"], "i": ["hi", "ci"], "f": ["hf", "cf"]}
+        tiles = [(gate, j) for gate in GATES for j in range(N_TILES)]
+        done = set()
+        grouped = {}
+        codes = {}
+        x_grouped = {}
+        x_codes = {}
+        turned_of = {}
         sums_of = {}
         biased_of = {}
         pre_of = {}
         gated_of = {}
-        rows_of = [slice(k * M_PER_BANK, (k + 1) * M_PER_BANK) for k in range(BANKS)]
-        cell = keep.tile([P, M_TILES, H], F32, name="cell")
+        bias_of = {}
+        cell = [keep.tile([P, M_TILES, P], F32, name="cell%d" % j) for j in range(N_TILES)]
+        kept = [keep.tile([P, M_TILES, P], F32, name="kept%d" % j) for j in range(N_TILES)]
         out_rows = out.rearrange("(p m) n -> p m n", m=M_TILES)
 
-        def regroup_weights(u, engine):
-            gate, chunk = units[u]
-            if u not in w_grouped_of:
-                w_grouped_of[u] = [
-                    regroup.tile([P, PASSES, CH, PACK], BF16, name="w_grouped", align_bytes=64)
-                    for product in products_of[gate]
-                ]
-            last_piece = len(products_of[gate]) * PASSES - 1
-            for w, (x_name, raw) in enumerate(products_of[gate]):
-                for g in range(PASSES):
-                    src = raw[:, g, :, chunk * CH : (chunk + 1) * CH].rearrange("p t (c i) -> p c t i", i=4)
-                    dst = w_grouped_of[u][w][:, g].rearrange("p (c i) t -> p c t i", i=4)
-                    if w * PASSES + g == last_piece and engine == "scalar":
-                        nc.scalar.copy(out=dst, in_=src)
-                    if w * PASSES + g != last_piece and engine == "vector":
-                        nc.vector.tensor_copy(out=dst, in_=src)
+        def regroup_part(key, engine):
+            name, g, half = key[:2], int(key[2]), "ab".index(key[3])
+            if key not in grouped:
+                grouped[key] = regroup.tile([P, HALF, PACK], BF16, name="w_grouped", align_bytes=64)
+            split = SV.get(key, SV[name])
+            lo, hi = (0, split) if engine == "V" else (split, HALF)
+            if lo == hi:
+                return
+            src = raw[key][:, :, lo:hi].rearrange("p t (c i) -> p c t i", i=4)
+            dst = grouped[key][:, lo:hi].rearrange("p (c i) t -> p c t i", i=4)
+            if engine == "V":
+                nc.vector.tensor_copy(out=dst, in_=src)
+            else:
+                nc.scalar.copy(out=dst, in_=src)
 
-        def quantise_weights(u):
-            w_quantised_of[u] = []
-            for w_grouped in w_grouped_of[u]:
-                w_codes = quantised.tile([P, PASSES * CH], U32, name="w_codes", align_bytes=64)
-                w_scales = quantised.tile([P, PASSES * CH], U8, name="w_scales", align_bytes=64)
+        def quantise_weight(key):
+            name, g = key[:2], int(key[2])
+            wk = name + key[3]
+            if wk not in codes:
+                w_codes = quantised.tile([P, PASSES * HALF], U32, name="w_codes", align_bytes=64)
+                w_scales = quantised.tile([P, PASSES * HALF], U8, name="w_scales", align_bytes=64)
+                codes[wk] = (w_codes, w_scales)
+            w_codes, w_scales = codes[wk]
+            cols = slice(g * HALF, (g + 1) * HALF)
+            nc.vector.quantize_mx(
+                out=w_codes[:, cols].bitcast(FP8X4),
+                scales=w_scales[:, cols],
+                in_=grouped[key][:].rearrange("p c t -> p (c t)"),
+            )
+
+        def turn_x(name, m):
+            words = rows[name][:, m, :].bitcast(F32).rearrange("p (g q u) -> p g u q", g=PASSES, u=2)
+            turned = psum_turn.tile([P, PASSES, 2, P], F32, name="turned")
+            for g in range(PASSES):
+                for u in range(2):
+                    nc.tensor.transpose(turned[:, g, u, :], words[:, g, u, :], ident_f32[:])
+            turned_of[name, m] = turned
+
+        def copy_x(name, m):
+            if name not in x_grouped:
+                x_grouped[name] = regroup.tile([P, PASSES, B, PACK], BF16, name="x_grouped", bufs=1, align_bytes=64)
+            nc.scalar.copy(
+                out=x_grouped[name][:, :, m * P : (m + 1) * P, :].bitcast(F32),
+                in_=turned_of[name, m][:].rearrange("p g u b -> p g b u"),
+            )
+
+        def quantise_x(name):
+            x_c = keep.tile([P, PASSES * B], U32, name=name + "_codes", align_bytes=64)
+            x_s = keep.tile([P, PASSES * B], U8, name=name + "_scales", align_bytes=64)
+            for g in range(PASSES):
                 nc.vector.quantize_mx(
-                    out=w_codes[:].bitcast(FP8X4),
-                    scales=w_scales[:],
-                    in_=w_grouped[:].rearrange("p g c t -> p (g c t)"),
+                    out=x_c[:, g * B : (g + 1) * B].bitcast(FP8X4),
+                    scales=x_s[:, g * B : (g + 1) * B],
+                    in_=x_grouped[name][:, g].rearrange("p b t -> p (b t)"),
                 )
-                w_quantised_of[u].append((w_codes, w_scales))
+            x_codes[name] = (x_c, x_s)
 
-        def multiply(u):
-            gate, chunk = units[u]
-            operands = []
-            for (x_name, raw), (w_codes, w_scales) in zip(products_of[gate], w_quantised_of[u]):
-                x_codes, x_scales = x_quantised[x_name]
+        def multiply(t):
+            gate, j = tiles[t]
+            sums = psum_sums.tile([P, B], F32, name="sums")
+            half, jj = divmod(j, N_TILES // 2)
+            names = products_of[gate]
+            for w, name in enumerate(names):
+                w_codes, w_scales = codes[name + "ab"[half]]
+                x_c, x_s = x_codes[name[0]]
                 for g in range(PASSES):
-                    operands.append((x_codes, x_scales, w_codes, w_scales, g))
-            sums_of[u] = []
-            for j in range(N_PER_CHUNK):
-                sums_t = psum_sums.tile([P, B], F32, name="sums_t")
-                for step, (x_codes, x_scales, w_codes, w_scales, g) in enumerate(operands):
-                    w_cols = slice(g * CH + j * P, g * CH + (j + 1) * P)
+                    w_cols = slice(g * HALF + jj * P, g * HALF + (jj + 1) * P)
                     x_cols = slice(g * B, (g + 1) * B)
                     nc.tensor.matmul_mx(
-                        out=sums_t[:],
+                        out=sums[:],
                         lhsT=w_codes[:, w_cols].bitcast(FP8X4),
                         lhsT_scale=w_scales[:, w_cols],
-                        rhs=x_codes[:, x_cols].bitcast(FP8X4),
-                        rhs_scale=x_scales[:, x_cols],
-                        start=(step == 0),
-                        stop=(step == len(operands) - 1),
+                        rhs=x_c[:, x_cols].bitcast(FP8X4),
+                        rhs_scale=x_s[:, x_cols],
+                        start=(w == 0 and g == 0),
+                        stop=(w == len(names) - 1 and g == PASSES - 1),
                     )
-                sums_of[u].append(sums_t)
+            sums_of[t] = sums
 
-        def add_bias(u):
-            gate, chunk = units[u]
-            biased_of[u] = []
-            for j, sums_t in enumerate(sums_of[u]):
-                biased = work.tile([P, B], F32, name="biased")
-                column = GATES.index(gate) * N_TILES + chunk * N_PER_CHUNK + j
-                nc.scalar.activation(
-                    out=biased[:], in_=sums_t[:], func=ACT.Identity, bias=bias_cols[:, column : column + 1]
+        def add_bias(t):
+            biased = work.tile([P, B], F32, name="biased")
+            nc.scalar.activation(
+                out=biased[:], in_=sums_of[t][:], func=ACT.Identity, bias=bias_of[0][:, t : t + 1]
+            )
+            biased_of[t] = biased
+
+        def turn_back(t):
+            gate, j = tiles[t]
+            pre = psum_pre.tile([P, M_TILES, P], F32, name="pre")
+            nc.tensor.matmul(
+                out=pre[:],
+                lhsT=ident_bf16[:],
+                rhs=rows["x" + gate][:, :, j * P : (j + 1) * P],
+                start=True,
+                stop=False,
+            )
+            for m in range(M_TILES):
+                nc.tensor.matmul(
+                    out=pre[:, m, :],
+                    lhsT=biased_of[t][:, m * P : (m + 1) * P],
+                    rhs=ident_f32[:],
+                    is_transpose=True,
+                    start=False,
+                    stop=(m == M_TILES - 1),
                 )
-                biased_of[u].append(biased)
+            pre_of[t] = pre
 
-        def turn_back_and_add_xz(u):
-            gate, chunk = units[u]
-            pre_of[u] = []
-            for k in range(BANKS):
-                pre = psum_pre.tile([P, M_PER_BANK, CH], F32, name="pre")
-                for s in range(M_PER_BANK):
-                    m = k * M_PER_BANK + s
-                    for j, biased in enumerate(biased_of[u]):
-                        nc.tensor.matmul(
-                            out=pre[:, s, j * P : (j + 1) * P],
-                            lhsT=biased[:, m * P : (m + 1) * P],
-                            rhs=ident_f32[:],
-                            is_transpose=True,
-                            start=(j == 0),
-                            stop=False,
-                        )
-                    nc.tensor.matmul(
-                        out=pre[:, s, :],
-                        lhsT=ident_bf16[:],
-                        rhs=xz_of[gate][:, m, chunk * CH : (chunk + 1) * CH],
-                        start=False,
-                        stop=True,
-                    )
-                pre_of[u].append(pre)
+        def activate(t):
+            gate, j = tiles[t]
+            cols = slice(j * P, (j + 1) * P)
+            if gate == "g":
+                nc.scalar.activation(out=cell[j][:], in_=pre_of[t][:], func=ACT.Tanh)
+            elif gate == "i":
+                nc.scalar.activation(out=kept[j][:], in_=pre_of[t][:], func=ACT.Sigmoid)
+            else:
+                gated = work.tile([P, M_TILES, P], F32, name="gated", bufs=WKG)
+                nc.scalar.activation(out=gated[:], in_=pre_of[t][:], func=ACT.Sigmoid)
+                gated_of[t] = gated
 
-        def activate(u):
-            gate, chunk = units[u]
-            cols = slice(chunk * CH, (chunk + 1) * CH)
-            gated_of[u] = []
-            for k, pre in enumerate(pre_of[u]):
-                if gate == "g":
-                    nc.scalar.activation(out=cell[:, rows_of[k], cols], in_=pre[:], func=ACT.Tanh)
-                else:
-                    gated = work.tile([P, M_PER_BANK, CH], F32, name="gated")
-                    nc.scalar.activation(out=gated[:], in_=pre[:], func=ACT.Sigmoid)
-                    gated_of[u].append(gated)
-
-        def combine(u):
-            gate, chunk = units[u]
-            cols = slice(chunk * CH, (chunk + 1) * CH)
+        def combine(t):
+            gate, j = tiles[t]
+            cols = slice(j * P, (j + 1) * P)
             if gate == "i":
-                for k, gated in enumerate(gated_of[u]):
-                    nc.vector.tensor_tensor(
-                        out=cell[:, rows_of[k], cols], in0=gated[:], in1=cell[:, rows_of[k], cols], op=ALU.mult
-                    )
-            if gate == "f":
-                for k, gated in enumerate(gated_of[u]):
-                    nc.vector.tensor_tensor(out=gated[:], in0=gated[:], in1=c_sb[:, rows_of[k], cols], op=ALU.mult)
-                for k, gated in enumerate(gated_of[u]):
-                    nc.vector.tensor_tensor(out=gated[:], in0=gated[:], in1=cell[:, rows_of[k], cols], op=ALU.add)
-                    nc.sync.dma_start(out=out_rows[:, rows_of[k], cols], in_=gated[:])
+                nc.vector.tensor_tensor(out=cell[j][:], in0=kept[j][:], in1=cell[j][:], op=ALU.mult)
+            if gate == "f" and t % 2 == 1:
+                for tt in (t - 1, t):
+                    cols = slice(tiles[tt][1] * P, (tiles[tt][1] + 1) * P)
+                    nc.vector.tensor_tensor(out=gated_of[tt][:], in0=gated_of[tt][:], in1=rows["c"][:, :, cols], op=ALU.mult)
+                for tt in (t - 1, t):
+                    cols = slice(tiles[tt][1] * P, (tiles[tt][1] + 1) * P)
+                    nc.vector.tensor_tensor(out=gated_of[tt][:], in0=gated_of[tt][:], in1=cell[tiles[tt][1]][:], op=ALU.add)
+                    nc.sync.dma_start(out=out_rows[:, :, cols], in_=gated_of[tt][:])
 
-        def make_ready(u):
-            for x_name, raw in products_of[units[u][0]]:
-                if x_name not in x_quantised:
-                    quantise_activation(x_name)
+        def bias_turn():
+            bias_t = psum_turn.tile([P, P], BF16, name="bias_t", tag="turned")
+            nc.tensor.transpose(bias_t[:], bias_rows[:], ident_bf16[:])
+            turned_of["bias"] = bias_t
 
-        def run(stage, u, *more):
-            if 0 <= u < len(units):
-                stage(u, *more)
+        def bias_copy():
+            bias_cols = keep.tile([P, len(GATES) * N_TILES], F32, name="bias_cols")
+            nc.scalar.copy(out=bias_cols[:], in_=turned_of["bias"][:, 0 : len(GATES) * N_TILES])
+            bias_of[0] = bias_cols
 
-        make_ready(0)
-        bias_t = psum_turn.tile([P, P], BF16, name="bias_t", tag="turned")
-        nc.tensor.transpose(bias_t[:], bias_rows[:], ident_bf16[:])
-        bias_cols = keep.tile([P, len(GATES) * N_TILES], F32, name="bias_cols")
-        nc.vector.tensor_copy(out=bias_cols[:], in_=bias_t[:, 0 : len(GATES) * N_TILES])
+        def vector_op(x):
+            if x[0] == "K":
+                t = int(x[1:])
+                return ("V" + x, ["SA" + x[1:]] + (["VK%d" % (t - N_TILES)] if tiles[t][0] == "f" else []), lambda: combine(t))
+            if x in ("qh", "qc"):
+                return ("V" + x, ["S%s%d" % (x[1], m) for m in range(M_TILES)], lambda: quantise_x(x[1]))
+            if x[0] == "q":
+                need = ["V" + x[1:]] + (["S" + x[1:]] if SV.get(x[1:], SV[x[1:3]]) < HALF else [])
+                return ("V" + x, need, lambda: quantise_weight(x[1:]))
+            return ("V" + x, [], lambda: regroup_part(x, "V"))
 
-        for step in range(len(units) + 4):
-            run(regroup_weights, step, "scalar")
-            run(quantise_weights, step - 1)
-            run(add_bias, step - 2)
-            run(turn_back_and_add_xz, step - 3)
-            run(multiply, step - 1)
-            run(activate, step - 3)
-            run(regroup_weights, step, "vector")
-            run(combine, step - 4)
-            run(make_ready, step + 1)
+        def scalar_op(x):
+            if x[0] == "B":
+                return ("S" + x, ["PM" + x[1:], "Sbias"], lambda: add_bias(int(x[1:])))
+            if x[0] == "A":
+                return ("S" + x, ["PT" + x[1:]], lambda: activate(int(x[1:])))
+            if x == "bias":
+                return ("Sbias", ["Pbias"], bias_copy)
+            if len(x) == 2:
+                return ("S" + x, ["P" + x], lambda: copy_x(x[0], int(x[1])))
+            return ("S" + x, [], lambda: regroup_part(x, "S"))
+
+        def tensor_op(x):
+            if x[0] == "M":
+                t = int(x[1:])
+                gate, j = tiles[t]
+                need = []
+                for name in products_of[gate]:
+                    need += ["Vq%s%d%s" % (name, g, "ab"[j // 4]) for g in range(PASSES)] + ["Vq" + name[0]]
+                return ("P" + x, need, lambda: multiply(t))
+            if x[0] == "T":
+                return ("P" + x, ["SB" + x[1:]], lambda: turn_back(int(x[1:])))
+            if x == "bias":
+                return ("Pbias", [], bias_turn)
+            return ("P" + x, [], lambda: turn_x(x[0], int(x[1])))
+
+        def expand(order):
+            flat = []
+            for x in order:
+                flat += [x[1] + str(m) for m in range(M_TILES)] if x in ("xh", "xc") else [x]
+            return flat
+
+        queues = [
+            [vector_op(x) for x in V_ORDER],
+            [scalar_op(x) for x in expand(S_ORDER)],
+            [tensor_op(x) for x in expand(PE_ORDER)],
+        ]
+        heads = [0, 0, 0]
+        moved = True
+        while moved:
+            moved = False
+            for q in range(3):
+                if heads[q] < len(queues[q]):
+                    token, needs, call = queues[q][heads[q]]
+                    if all(n in done for n in needs):
+                        call()
+                        done.add(token)
+                        heads[q] += 1
+                        moved = True
+        assert all(heads[q] == len(queues[q]) for q in range(3)), [queues[q][heads[q]][0:2] for q in range(3) if heads[q] < len(queues[q])]

@@ -22,15 +22,16 @@ HALF = H // 2
 FLOPS = 2 * B * H * H * 5
 
 GATES = ("g", "i", "f")
-LOADS = "hg0a h hg1a bias hg0b hg1b hi0a xg hi1a c ci0a ci1a hi0b hi1b ci0b ci1b xi hf0 hf1 cf0 cf1 xf".split()
-SV = {"hg": 384, "hg0a": 256, "hi": 416, "ci": 416, "hf": 352, "cf": 384}
-NSUM, NPRE, NTURN, WG, WQ, WKB, WKG = 4, 2, 2, 4, 5, 4, 4
+LOADS = "hg0a h01 h23 hg1a bias hg0b hg1b hi0a xg hi1a c ci0a ci1a hi0b hi1b ci0b ci1b xi hf0 hf1 cf0 cf1 xf".split()
+SV = {"hg": 320, "hg0a": 512, "hg1a": 448, "hi": 416, "ci": 448, "hf": 352, "cf": 384}
+NSUM, NPRE, WG, WQ, WKB, WIDE = 4, 4, 4, 5, 6, 0
+DUMMY = 3
 A_LAG = 2
 T_LAG = 2
 K_LAG = 3
-V_ORDER = "hg0a qhg0a hg1a hg0b qh qhg1a hg1b qhg0b hi0a qhg1b hi1a qhi0a qhi1a qc ci0a ci1a qci0a hi0b qci1a hi1b qhi0b ci0b qhi1b ci1b qci0b hf0a qci1b hf1a qhf0a K8 qhf1a cf0a K9 cf1a qcf0a hf0b qcf1a hf1b qhf0b K10 qhf1b cf0b K11 cf1b qcf0b K12 qcf1b K13 K14 K15 K16 K17 K18 K19 K20 K21 K22 K23".split()
-S_ORDER = "hg0a xh hg1a bias hg0b hg1b B0 B1 hi0a B2 B3 A0 A1 hi1a xc B4 B5 A2 A3 ci0a ci1a B6 B7 A4 A5 hi0b hi1b A6 A7 B8 B9 ci0b ci1b B10 B11 A8 A9 hf0a hf1a B12 B13 A10 A11 cf0a cf1a B14 B15 A12 A13 hf0b hf1b A14 A15 B16 B17 cf0b cf1b B18 B19 A16 A17 B20 B21 A18 A19 B22 B23 A20 A21 A22 A23".split()
-PE_ORDER = "xh bias M0 M1 M2 M3 T0 T1 xc M4 M5 T2 T3 M6 M7 T4 T5 T6 T7 M8 M9 M10 M11 T8 T9 M12 M13 T10 T11 M14 M15 T12 T13 T14 T15 M16 M17 M18 M19 T16 T17 M20 M21 T18 T19 M22 M23 T20 T21 T22 T23".split()
+V_ORDER = "hg0a qhg0a hg1a qh0 qh1 qhg1a hg0b hg1b qhg0b hi0a qhg1b qhi0a hi1a qhi1a ci0a ci1a qc0 hi0b qc1 hi1b qci0a qci1a qhi0b ci0b qhi1b ci1b qci0b hf0a qci1b K9 hf1a qhf0a qhf1a cf0a K11 cf1a qcf0a hf0b qcf1a hf1b qhf0b qhf1b cf0b cf1b qcf0b K13 qcf1b K15 K17 K19 K21 K23".split()
+S_ORDER = "h0 h2 h1 h3 hg0a hg1a bias hg0b hg1b B0 B1 hi0a B2 B3 A0 hi1a A1 B4 B5 B6 B7 xc A2 A3 ci0a ci1a A4 A5 hi0b hi1b A6 A7 B8 B9 ci0b ci1b B10 B11 A8 A9 hf0a hf1a B12 B13 A10 A11 cf0a B14 cf1a B15 A12 A13 hf0b hf1b A14 A15 B16 B17 cf0b cf1b B18 B19 A16 A17 B20 B21 A18 A19 B22 B23 A20 A21 A22 A23".split()
+PE_ORDER = "dummy h0 h2 h1 h3 bias M0:0 M1:0 M2:0 M3:0 M0:1 M1:1 M2:1 M3:1 T0 T1 M4 M5 M6 M7 xc T2 T3 T4 T5 T6 T7 M8:0-1 M9:0-1 M10:0-1 M8:2-3 M9:2-3 M10:2-3 M11 T8 T9 M12:0-1 M13:0-1 M12:2-3 M13:2-3 T10 T11 M14 M15 T12 T13 T14 T15 M16:0-1 M17:0-1 M16:2-3 M17:2-3 M18 M19 T16 T17 M20:0-1 M21:0-1 M20:2-3 M21:2-3 T18 T19 M22 M23 T20 T21 T22 T23".split()
 
 
 def tile_residuallstmcell_pa_kernel(
@@ -42,7 +43,6 @@ def tile_residuallstmcell_pa_kernel(
         regroup = stack.enter_context(tc.tile_pool(name="regroup", bufs=WG))
         quantised = stack.enter_context(tc.tile_pool(name="quantised", bufs=WQ))
         work = stack.enter_context(tc.tile_pool(name="work", bufs=WKB))
-        psum_turn = stack.enter_context(tc.psum_pool(name="psum_turn", bufs=NTURN))
         psum_sums = stack.enter_context(tc.psum_pool(name="psum_sums", bufs=NSUM))
         psum_pre = stack.enter_context(tc.psum_pool(name="psum_pre", bufs=NPRE))
         stack.enter_context(tc.manual_schedule())
@@ -61,6 +61,7 @@ def tile_residuallstmcell_pa_kernel(
         rows_dram = {"h": h_prev, "c": c_prev, "xg": xz_g, "xi": xz_i, "xf": xz_f}
         bias_dram = {"g": b_g, "i": b_i, "f": b_f}
         raw = {}
+        x_pair = {}
         rows = {}
         for item in LOADS:
             if item == "bias":
@@ -72,6 +73,13 @@ def tile_residuallstmcell_pa_kernel(
             elif item in rows_dram:
                 rows[item] = keep.tile([P, M_TILES, H], BF16, name=item + "_rows")
                 nc.sync.dma_start(out=rows[item][:], in_=rows_dram[item].rearrange("(p m) n -> p m n", m=M_TILES))
+            elif item in ("h01", "h23"):
+                m0 = int(item[1])
+                x_pair[item] = keep.tile([P, 2, H], BF16, name=item + "_rows")
+                nc.sync.dma_start(
+                    out=x_pair[item][:],
+                    in_=h_prev.rearrange("(p m) n -> p m n", m=M_TILES)[:, m0 : m0 + 2, :],
+                )
             else:
                 name, g = item[:2], int(item[2])
                 cols = {"": slice(0, H), "a": slice(0, HALF), "b": slice(HALF, H)}[item[3:]]
@@ -97,8 +105,10 @@ def tile_residuallstmcell_pa_kernel(
         pre_of = {}
         gated_of = {}
         bias_of = {}
-        cell = [keep.tile([P, M_TILES, P], F32, name="cell%d" % j) for j in range(N_TILES)]
-        kept = [keep.tile([P, M_TILES, P], F32, name="kept%d" % j) for j in range(N_TILES)]
+        cell2 = [keep.tile([P, 2, M_TILES, P], F32, name="cell%d" % j) for j in range(N_TILES // 2)]
+        kept2 = [keep.tile([P, 2, M_TILES, P], F32, name="kept%d" % j) for j in range(N_TILES // 2)]
+        cell = [cell2[j // 2][:, j % 2] for j in range(N_TILES)]
+        kept = [kept2[j // 2][:, j % 2] for j in range(N_TILES)]
         out_rows = out.rearrange("(p m) n -> p m n", m=M_TILES)
 
         def regroup_part(key, engine):
@@ -131,42 +141,53 @@ def tile_residuallstmcell_pa_kernel(
                 in_=grouped[key][:].rearrange("p c t -> p (c t)"),
             )
 
-        def turn_x(name, m):
-            words = rows[name][:, m, :].bitcast(F32).rearrange("p (g q u) -> p g u q", g=PASSES, u=2)
-            turned = psum_turn.tile([P, PASSES, 2, P], F32, name="turned")
-            for g in range(PASSES):
+        def turn_x(name, k):
+            g, pair = divmod(k, 2)
+            turned = psum_pre.tile([P, 2, 2, P], F32, name="turned", tag="pre")
+            for m in range(2):
+                src = x_pair["h01" if pair == 0 else "h23"][:, m, :] if name == "h" and x_pair else rows[name][:, 2 * pair + m, :]
+                words = src.bitcast(F32).rearrange("p (g q u) -> p g u q", g=PASSES, u=2)
                 for u in range(2):
-                    nc.tensor.transpose(turned[:, g, u, :], words[:, g, u, :], ident_f32[:])
-            turned_of[name, m] = turned
+                    nc.tensor.transpose(turned[:, m, u, :], words[:, g, u, :], ident_f32[:])
+            turned_of[name, k] = turned
 
-        def copy_x(name, m):
-            if name not in x_grouped:
-                x_grouped[name] = regroup.tile([P, PASSES, B, PACK], BF16, name="x_grouped", bufs=1, align_bytes=64)
-            nc.scalar.copy(
-                out=x_grouped[name][:, :, m * P : (m + 1) * P, :].bitcast(F32),
-                in_=turned_of[name, m][:].rearrange("p g u b -> p g b u"),
+        def copy_x(name, k, engine):
+            g, pair = divmod(k, 2)
+            if (name, g) not in x_grouped:
+                x_grouped[name, g] = regroup.tile([P, B, PACK], BF16, name="x_grouped%d" % g, bufs=1, align_bytes=64)
+            copy = nc.vector.tensor_copy if engine == "V" else nc.scalar.copy
+            copy(
+                out=x_grouped[name, g][:, pair * 2 * P : (pair + 1) * 2 * P, :].bitcast(F32).rearrange("p (m b) u -> p m b u", m=2),
+                in_=turned_of[name, k][:].rearrange("p m u b -> p m b u"),
             )
 
-        def quantise_x(name):
-            x_c = keep.tile([P, PASSES * B], U32, name=name + "_codes", align_bytes=64)
-            x_s = keep.tile([P, PASSES * B], U8, name=name + "_scales", align_bytes=64)
-            for g in range(PASSES):
-                nc.vector.quantize_mx(
-                    out=x_c[:, g * B : (g + 1) * B].bitcast(FP8X4),
-                    scales=x_s[:, g * B : (g + 1) * B],
-                    in_=x_grouped[name][:, g].rearrange("p b t -> p (b t)"),
+        def quantise_x(name, g):
+            if name not in x_codes:
+                x_codes[name] = (
+                    keep.tile([P, PASSES * B], U32, name=name + "_codes", align_bytes=64),
+                    keep.tile([P, PASSES * B], U8, name=name + "_scales", align_bytes=64),
                 )
-            x_codes[name] = (x_c, x_s)
+            x_c, x_s = x_codes[name]
+            nc.vector.quantize_mx(
+                out=x_c[:, g * B : (g + 1) * B].bitcast(FP8X4),
+                scales=x_s[:, g * B : (g + 1) * B],
+                in_=x_grouped[name, g][:].rearrange("p b t -> p (b t)"),
+            )
 
-        def multiply(t):
+        def passes_of(t):
+            return [(name, g) for name in products_of[tiles[t][0]] for g in range(PASSES)]
+
+        def multiply(t, steps):
             gate, j = tiles[t]
-            sums = psum_sums.tile([P, B], F32, name="sums")
+            if steps[0] == 0:
+                sums_of[t] = psum_sums.tile([P, B], F32, name="sums")
+            sums = sums_of[t]
             half, jj = divmod(j, N_TILES // 2)
-            names = products_of[gate]
-            for w, name in enumerate(names):
-                w_codes, w_scales = codes[name + "ab"[half]]
-                x_c, x_s = x_codes[name[0]]
-                for g in range(PASSES):
+            if True:
+                for step in steps:
+                    name, g = passes_of(t)[step]
+                    w_codes, w_scales = codes[name + "ab"[half]]
+                    x_c, x_s = x_codes[name[0]]
                     w_cols = slice(g * HALF + jj * P, g * HALF + (jj + 1) * P)
                     x_cols = slice(g * B, (g + 1) * B)
                     nc.tensor.matmul_mx(
@@ -175,10 +196,9 @@ def tile_residuallstmcell_pa_kernel(
                         lhsT_scale=w_scales[:, w_cols],
                         rhs=x_c[:, x_cols].bitcast(FP8X4),
                         rhs_scale=x_s[:, x_cols],
-                        start=(w == 0 and g == 0),
-                        stop=(w == len(names) - 1 and g == PASSES - 1),
+                        start=(step == 0),
+                        stop=(step == len(passes_of(t)) - 1),
                     )
-            sums_of[t] = sums
 
         def add_bias(t):
             biased = work.tile([P, B], F32, name="biased")
@@ -212,30 +232,39 @@ def tile_residuallstmcell_pa_kernel(
             gate, j = tiles[t]
             cols = slice(j * P, (j + 1) * P)
             if gate == "g":
-                nc.scalar.activation(out=cell[j][:], in_=pre_of[t][:], func=ACT.Tanh)
-            elif gate == "i":
-                nc.scalar.activation(out=kept[j][:], in_=pre_of[t][:], func=ACT.Sigmoid)
+                nc.scalar.activation(out=cell[j], in_=pre_of[t][:], func=ACT.Tanh)
             else:
-                gated = work.tile([P, M_TILES, P], F32, name="gated", bufs=WKG)
-                nc.scalar.activation(out=gated[:], in_=pre_of[t][:], func=ACT.Sigmoid)
-                gated_of[t] = gated
+                nc.scalar.activation(out=kept[j], in_=pre_of[t][:], func=ACT.Sigmoid)
+                gated_of[t] = kept[j]
 
         def combine(t):
             gate, j = tiles[t]
-            cols = slice(j * P, (j + 1) * P)
+            if j % 2 == 0:
+                return
             if gate == "i":
-                nc.vector.tensor_tensor(out=cell[j][:], in0=kept[j][:], in1=cell[j][:], op=ALU.mult)
-            if gate == "f" and t % 2 == 1:
-                for tt in (t - 1, t):
-                    cols = slice(tiles[tt][1] * P, (tiles[tt][1] + 1) * P)
-                    nc.vector.tensor_tensor(out=gated_of[tt][:], in0=gated_of[tt][:], in1=rows["c"][:, :, cols], op=ALU.mult)
-                for tt in (t - 1, t):
-                    cols = slice(tiles[tt][1] * P, (tiles[tt][1] + 1) * P)
-                    nc.vector.tensor_tensor(out=gated_of[tt][:], in0=gated_of[tt][:], in1=cell[tiles[tt][1]][:], op=ALU.add)
-                    nc.sync.dma_start(out=out_rows[:, :, cols], in_=gated_of[tt][:])
+                nc.vector.tensor_tensor(out=cell2[j // 2][:], in0=kept2[j // 2][:], in1=cell2[j // 2][:], op=ALU.mult)
+            if gate == "f":
+                k2, c2 = kept2[j // 2], cell2[j // 2]
+                c_cols = rows["c"][:, :, (j - 1) * P : (j + 1) * P].rearrange("p m (j n) -> p j m n", j=2)
+                if t < WIDE:
+                    nc.vector.tensor_tensor(out=k2[:], in0=k2[:], in1=c_cols, op=ALU.mult)
+                    nc.vector.tensor_tensor(out=k2[:], in0=k2[:], in1=c2[:], op=ALU.add)
+                    for e in range(2):
+                        nc.sync.dma_start(out=out_rows[:, :, (j - 1 + e) * P : (j + e) * P], in_=k2[:, e])
+                else:
+                    for e in range(2):
+                        nc.vector.tensor_tensor(out=k2[:, e], in0=k2[:, e], in1=c_cols[:, e], op=ALU.mult)
+                    for e in range(2):
+                        nc.vector.tensor_tensor(out=k2[:, e], in0=k2[:, e], in1=c2[:, e], op=ALU.add)
+                        nc.sync.dma_start(out=out_rows[:, :, (j - 1 + e) * P : (j + e) * P], in_=k2[:, e])
+
+        def warm_up():
+            idle = psum_pre.tile([P, B], F32, name="idle", tag="pre")
+            for k in range(DUMMY):
+                nc.tensor.matmul(out=idle[:], lhsT=ident_bf16[:], rhs=raw["hg0a"][:, k, :], start=True, stop=True)
 
         def bias_turn():
-            bias_t = psum_turn.tile([P, P], BF16, name="bias_t", tag="turned")
+            bias_t = psum_pre.tile([P, P], BF16, name="bias_t", tag="pre")
             nc.tensor.transpose(bias_t[:], bias_rows[:], ident_bf16[:])
             turned_of["bias"] = bias_t
 
@@ -248,8 +277,11 @@ def tile_residuallstmcell_pa_kernel(
             if x[0] == "K":
                 t = int(x[1:])
                 return ("V" + x, ["SA" + x[1:]] + (["VK%d" % (t - N_TILES)] if tiles[t][0] == "f" else []), lambda: combine(t))
-            if x in ("qh", "qc"):
-                return ("V" + x, ["S%s%d" % (x[1], m) for m in range(M_TILES)], lambda: quantise_x(x[1]))
+            if len(x) == 2 and x[1] in "0123":
+                return ("C" + x, ["P" + x], lambda: copy_x(x[0], int(x[1]), "V"))
+            if x[:2] in ("qh", "qc") and len(x) == 3:
+                g = int(x[2])
+                return ("V" + x, ["C%s%d" % (x[1], 2 * g + e) for e in range(2)], lambda: quantise_x(x[1], g))
             if x[0] == "q":
                 need = ["V" + x[1:]] + (["S" + x[1:]] if SV.get(x[1:], SV[x[1:3]]) < HALF else [])
                 return ("V" + x, need, lambda: quantise_weight(x[1:]))
@@ -263,19 +295,25 @@ def tile_residuallstmcell_pa_kernel(
             if x == "bias":
                 return ("Sbias", ["Pbias"], bias_copy)
             if len(x) == 2:
-                return ("S" + x, ["P" + x], lambda: copy_x(x[0], int(x[1])))
+                return ("C" + x, ["P" + x], lambda: copy_x(x[0], int(x[1]), "S"))
             return ("S" + x, [], lambda: regroup_part(x, "S"))
 
         def tensor_op(x):
             if x[0] == "M":
-                t = int(x[1:])
-                gate, j = tiles[t]
+                t, part = x[1:].split(":") if ":" in x else (x[1:], "0-%d" % (len(passes_of(int(x[1:]))) - 1))
+                t = int(t)
+                lo, hi = part.split("-") if "-" in part else (part, part)
+                steps = list(range(int(lo), int(hi) + 1))
                 need = []
-                for name in products_of[gate]:
-                    need += ["Vq%s%d%s" % (name, g, "ab"[j // 4]) for g in range(PASSES)] + ["Vq" + name[0]]
-                return ("P" + x, need, lambda: multiply(t))
+                for step in steps:
+                    name, g = passes_of(t)[step]
+                    need += ["Vq%s%d%s" % (name, g, "ab"[tiles[t][1] // 4]), "Vq%s%d" % (name[0], g)]
+                last = steps[-1] == len(passes_of(t)) - 1
+                return ("PM%d" % t if last else "P" + x, need, lambda: multiply(t, steps))
             if x[0] == "T":
                 return ("P" + x, ["SB" + x[1:]], lambda: turn_back(int(x[1:])))
+            if x == "dummy":
+                return ("Pdummy", [], warm_up)
             if x == "bias":
                 return ("Pbias", [], bias_turn)
             return ("P" + x, [], lambda: turn_x(x[0], int(x[1])))

@@ -31,7 +31,7 @@ T_LAG = 2
 K_LAG = 3
 V_ORDER = "hg0a qhg0a hg1a qh0 qh1 qhg1a hg0b hg1b qhg0b hi0a qhg1b qhi0a hi1a qhi1a ci0a ci1a qc0 hi0b qc1 hi1b qci0a qci1a qhi0b ci0b qhi1b ci1b qci0b hf0a qci1b K9 hf1a qhf0a qhf1a cf0a K11 cf1a qcf0a hf0b qcf1a hf1b qhf0b qhf1b cf0b cf1b qcf0b K13 qcf1b K15 K17 K19 K21 K23".split()
 S_ORDER = "h0 h2 h1 h3 hg0a hg1a bias hg0b hg1b B0 B1 hi0a B2 B3 A0 hi1a A1 B4 B5 B6 B7 xc A2 A3 ci0a ci1a A4 A5 hi0b hi1b A6 A7 B8 B9 ci0b ci1b B10 B11 A8 A9 hf0a hf1a B12 B13 A10 A11 cf0a B14 cf1a B15 A12 A13 hf0b hf1b A14 A15 B16 B17 cf0b cf1b B18 B19 A16 A17 B20 B21 A18 A19 B22 B23 A20 A21 A22 A23".split()
-PE_ORDER = "dummy h0 h2 h1 h3 bias M0:0 M1:0 M2:0 M3:0 M0:1 M1:1 M2:1 M3:1 T0 T1 M4 M5 M6 M7 xc T2 T3 T4 T5 T6 T7 M8:0-1 M9:0-1 M10:0-1 M8:2-3 M9:2-3 M10:2-3 M11 T8 T9 M12:0-1 M13:0-1 M12:2-3 M13:2-3 T10 T11 M14 M15 T12 T13 T14 T15 M16:0-1 M17:0-1 M16:2-3 M17:2-3 M18 M19 T16 T17 M20:0-1 M21:0-1 M20:2-3 M21:2-3 T18 T19 M22 M23 T20 T21 T22 T23".split()
+PE_ORDER = "dummy h0 h2 h1 h3 bias M0:0 M1:0 M2:0 M3:0 M0:1 M1:1 M2:1 M3:1 I0 I1 T0 T1 M4 M5 M6 M7 xc I2 I3 T2 T3 I4 I5 T4 T5 I6 I7 T6 T7 M8:0-1 M9:0-1 M10:0-1 M8:2-3 M9:2-3 M10:2-3 M11 I8 I9 T8 T9 M12:0-1 M13:0-1 M12:2-3 M13:2-3 I10 I11 T10 T11 M14 M15 I12 I13 T12 T13 I14 I15 T14 T15 M16:0-1 M17:0-1 M16:2-3 M17:2-3 M18 M19 I16 I17 T16 T17 M20:0-1 M21:0-1 M20:2-3 M21:2-3 I18 I19 T18 T19 M22 M23 I20 I21 T20 T21 I22 I23 T22 T23".split()
 
 
 def tile_residuallstmcell_pa_kernel(
@@ -207,7 +207,7 @@ def tile_residuallstmcell_pa_kernel(
             )
             biased_of[t] = biased
 
-        def turn_back(t):
+        def open_with_xz(t):
             gate, j = tiles[t]
             pre = psum_pre.tile([P, M_TILES, P], F32, name="pre")
             nc.tensor.matmul(
@@ -217,16 +217,18 @@ def tile_residuallstmcell_pa_kernel(
                 start=True,
                 stop=False,
             )
+            pre_of[t] = pre
+
+        def turn_back(t):
             for m in range(M_TILES):
                 nc.tensor.matmul(
-                    out=pre[:, m, :],
+                    out=pre_of[t][:, m, :],
                     lhsT=biased_of[t][:, m * P : (m + 1) * P],
                     rhs=ident_f32[:],
                     is_transpose=True,
                     start=False,
                     stop=(m == M_TILES - 1),
                 )
-            pre_of[t] = pre
 
         def activate(t):
             gate, j = tiles[t]
@@ -312,6 +314,8 @@ def tile_residuallstmcell_pa_kernel(
                 return ("PM%d" % t if last else "P" + x, need, lambda: multiply(t, steps))
             if x[0] == "T":
                 return ("P" + x, ["SB" + x[1:]], lambda: turn_back(int(x[1:])))
+            if x[0] == "I":
+                return ("P" + x, [], lambda: open_with_xz(int(x[1:])))
             if x == "dummy":
                 return ("Pdummy", [], warm_up)
             if x == "bias":

@@ -31,7 +31,7 @@ T_LAG = 2
 K_LAG = 3
 V_ORDER = "hg0a qhg0a hg1a qh0 qh1 qhg1a hg0b hg1b qhg0b hi0a qhg1b qhi0a hi1a qhi1a ci0a ci1a qc0 hi0b qc1 hi1b qci0a qci1a qhi0b ci0b qhi1b ci1b qci0b hf0a qci1b K9 hf1a qhf0a qhf1a cf0a K11 cf1a qcf0a hf0b qcf1a hf1b qhf0b qhf1b cf0b cf1b qcf0b K13 qcf1b K15 K17 K19 K21 K23".split()
 S_ORDER = "h0 h2 h1 h3 hg0a hg1a bias hg0b hg1b B0 B1 hi0a B2 B3 A0 hi1a A1 B4 B5 B6 B7 xc A2 A3 ci0a ci1a A4 A5 hi0b hi1b A6 A7 B8 B9 ci0b ci1b B10 B11 A8 A9 hf0a hf1a B12 B13 A10 A11 cf0a B14 cf1a B15 A12 A13 hf0b hf1b A14 A15 B16 B17 cf0b cf1b B18 B19 A16 A17 B20 B21 A18 A19 B22 B23 A20 A21 A22 A23".split()
-PE_ORDER = "dummy h0 h2 h1 h3 bias M0:0 M1:0 M2:0 M3:0 M0:1 M1:1 M2:1 M3:1 I0 I1 T0 T1 M4 M5 M6 M7 xc I2 I3 T2 T3 I4 I5 T4 T5 I6 I7 T6 T7 M8:0-1 M9:0-1 M10:0-1 M8:2-3 M9:2-3 M10:2-3 M11 I8 I9 T8 T9 M12:0-1 M13:0-1 M12:2-3 M13:2-3 I10 I11 T10 T11 M14 M15 I12 I13 T12 T13 I14 I15 T14 T15 M16:0-1 M17:0-1 M16:2-3 M17:2-3 M18 M19 I16 I17 T16 T17 M20:0-1 M21:0-1 M20:2-3 M21:2-3 I18 I19 T18 T19 M22 M23 I20 I21 T20 T21 I22 I23 T22 T23".split()
+PE_ORDER = "dd3 h0 h2 h1 h3 bias dd4 M0:0 M1:0 M2:0 M3:0 M0:1 M1:1 M2:1 M3:1 I0 I1 T0 T1 M4 M5 M6 M7 xc I2 I3 T2 T3 I4 I5 T4 T5 I6 I7 T6 T7 M8:0-1 M9:0-1 M10:0-1 M8:2-3 M9:2-3 M10:2-3 M11 I8 I9 T8 T9 M12:0-1 M13:0-1 M12:2-3 M13:2-3 I10 I11 T10 T11 M14 M15 I12 I13 T12 T13 I14 I15 T14 T15 M16:0-1 M17:0-1 M16:2-3 M17:2-3 M18 M19 I16 I17 T16 T17 M20:0-1 M21:0-1 M20:2-3 M21:2-3 I18 I19 T18 T19 M22 M23 I20 I21 T20 T21 I22 I23 T22 T23".split()
 
 
 def tile_residuallstmcell_pa_kernel(
@@ -260,10 +260,10 @@ def tile_residuallstmcell_pa_kernel(
                         nc.vector.tensor_tensor(out=k2[:, e], in0=k2[:, e], in1=c2[:, e], op=ALU.add)
                         nc.sync.dma_start(out=out_rows[:, :, (j - 1 + e) * P : (j + e) * P], in_=k2[:, e])
 
-        def warm_up():
+        def warm_up(count):
             idle = psum_pre.tile([P, B], F32, name="idle", tag="pre")
-            for k in range(DUMMY):
-                nc.tensor.matmul(out=idle[:], lhsT=ident_bf16[:], rhs=raw["hg0a"][:, k, :], start=True, stop=True)
+            for k in range(count):
+                nc.tensor.matmul(out=idle[:], lhsT=ident_bf16[:], rhs=raw["hg0a"][:, k % PACK, :], start=True, stop=True)
 
         def bias_turn():
             bias_t = psum_pre.tile([P, P], BF16, name="bias_t", tag="pre")
@@ -316,8 +316,8 @@ def tile_residuallstmcell_pa_kernel(
                 return ("P" + x, ["SB" + x[1:]], lambda: turn_back(int(x[1:])))
             if x[0] == "I":
                 return ("P" + x, [], lambda: open_with_xz(int(x[1:])))
-            if x == "dummy":
-                return ("Pdummy", [], warm_up)
+            if x[:2] == "dd":
+                return ("P" + x, [], lambda: warm_up(int(x[2])))
             if x == "bias":
                 return ("Pbias", [], bias_turn)
             return ("P" + x, [], lambda: turn_x(x[0], int(x[1])))

from contextlib import ExitStack

import concourse.mybir as mybir
from concourse.masks import make_identity

F32 = mybir.dt.float32
BF16 = mybir.dt.bfloat16
U32 = mybir.dt.uint32
U8 = mybir.dt.uint8
FP8X4 = mybir.dt.float8_e4m3fn_x4
ACT = mybir.ActivationFunctionType
ALU = mybir.AluOpType
P = 128
PACK = 4
K_PASS = P * PACK
B = 512
H = 1024
M_TILES = B // P
N_TILES = H // P
PASSES = H // K_PASS
HALF = H // 2
FLOPS = 2 * B * H * H * 5

GATES = ("g", "i", "f")
LOADS = "hg0a h01 h23 hg1a bias hg0b hg1b hi0a xg hi1a c ci0a ci1a hi0b hi1b ci0b ci1b xi hf0 hf1 cf0 cf1 xf".split()
SV = {"hg": 320, "hg0a": 512, "hg1a": 448, "hi": 416, "ci": 448, "hf": 352, "cf": 384}
NSUM, NPRE, WG, WQ, WKB, WIDE = 4, 4, 4, 5, 6, 0
DUMMY = 3
A_LAG = 2
T_LAG = 2
K_LAG = 3
V_ORDER = "hg0a qhg0a hg1a qh0 qh1 qhg1a hg0b hg1b qhg0b hi0a qhg1b qhi0a hi1a qhi1a ci0a ci1a qc0 hi0b qc1 hi1b qci0a qci1a qhi0b ci0b qhi1b ci1b qci0b hf0a qci1b K9 hf1a qhf0a qhf1a cf0a K11 cf1a qcf0a hf0b qcf1a hf1b qhf0b qhf1b cf0b cf1b qcf0b K13 qcf1b K15 K17 K19 K21 K23".split()
S_ORDER = "h0 h2 h1 h3 hg0a hg1a bias hg0b hg1b B0 B1 hi0a B2 B3 A0 hi1a A1 B4 B5 B6 B7 xc A2 A3 ci0a ci1a A4 A5 hi0b hi1b A6 A7 B8 B9 ci0b ci1b B10 B11 A8 A9 hf0a hf1a B12 B13 A10 A11 cf0a B14 cf1a B15 A12 A13 hf0b hf1b A14 A15 B16 B17 cf0b cf1b B18 B19 A16 A17 B20 B21 A18 A19 B22 B23 A20 A21 A22 A23".split()
PE_ORDER = "dd3 h0 h2 h1 h3 bias dd4 M0:0 M1:0 M2:0 M3:0 M0:1 M1:1 M2:1 M3:1 I0 I1 T0 T1 M4 M5 M6 M7 xc I2 I3 T2 T3 I4 I5 T4 T5 I6 I7 T6 T7 M8:0-1 M9:0-1 M10:0-1 M8:2-3 M9:2-3 M10:2-3 M11 I8 I9 T8 T9 M12:0-1 M13:0-1 M12:2-3 M13:2-3 I10 I11 T10 T11 M14 M15 I12 I13 T12 T13 I14 I15 T14 T15 M16:0-1 M17:0-1 M16:2-3 M17:2-3 M18 M19 I16 I17 T16 T17 M20:0-1 M21:0-1 M20:2-3 M21:2-3 I18 I19 T18 T19 M22 M23 I20 I21 T20 T21 I22 I23 T22 T23".split()


def tile_residuallstmcell_pa_kernel(
    tc, xz_i, xz_f, xz_g, h_prev, c_prev, w_hi, w_ci, w_hf, w_cf, w_hg, b_i, b_f, b_g, out
):
    nc = tc.nc
    with ExitStack() as stack:
        keep = stack.enter_context(tc.tile_pool(name="keep", bufs=1))
        regroup = stack.enter_context(tc.tile_pool(name="regroup", bufs=WG))
        quantised = stack.enter_context(tc.tile_pool(name="quantised", bufs=WQ))
        work = stack.enter_context(tc.tile_pool(name="work", bufs=WKB))
        psum_sums = stack.enter_context(tc.psum_pool(name="psum_sums", bufs=NSUM))
        psum_pre = stack.enter_context(tc.psum_pool(name="psum_pre", bufs=NPRE))
        stack.enter_context(tc.manual_schedule())

        warm = keep.tile([P, 1], F32, name="warm")
        nc.vector.memset(warm[:], 0.0)
        nc.scalar.activation(out=warm[:], in_=warm[:], func=ACT.Sigmoid)
        bias_rows = keep.tile([P, P], BF16, name="bias_rows")
        nc.vector.memset(bias_rows[:], 0.0)
        ident_f32 = keep.tile([P, P], F32, name="ident_f32")
        make_identity(nc, ident_f32[:])
        ident_bf16 = keep.tile([P, P], BF16, name="ident_bf16")
        make_identity(nc, ident_bf16[:])

        w_dram = {"hg": w_hg, "hi": w_hi, "ci": w_ci, "hf": w_hf, "cf": w_cf}
        rows_dram = {"h": h_prev, "c": c_prev, "xg": xz_g, "xi": xz_i, "xf": xz_f}
        bias_dram = {"g": b_g, "i": b_i, "f": b_f}
        raw = {}
        x_pair = {}
        rows = {}
        for item in LOADS:
            if item == "bias":
                for q, gate in enumerate(GATES):
                    nc.sync.dma_start(
                        out=bias_rows[q * N_TILES : (q + 1) * N_TILES, :],
                        in_=bias_dram[gate].rearrange("(j p) -> j p", p=P),
                    )
            elif item in rows_dram:
                rows[item] = keep.tile([P, M_TILES, H], BF16, name=item + "_rows")
                nc.sync.dma_start(out=rows[item][:], in_=rows_dram[item].rearrange("(p m) n -> p m n", m=M_TILES))
            elif item in ("h01", "h23"):
                m0 = int(item[1])
                x_pair[item] = keep.tile([P, 2, H], BF16, name=item + "_rows")
                nc.sync.dma_start(
                    out=x_pair[item][:],
                    in_=h_prev.rearrange("(p m) n -> p m n", m=M_TILES)[:, m0 : m0 + 2, :],
                )
            else:
                name, g = item[:2], int(item[2])
                cols = {"": slice(0, H), "a": slice(0, HALF), "b": slice(HALF, H)}[item[3:]]
                width = cols.stop - cols.start
                piece = keep.tile([P, PACK, width], BF16, name="raw_" + item)
                nc.sync.dma_start(
                    out=piece[:],
                    in_=w_dram[name][g * K_PASS : (g + 1) * K_PASS, cols].rearrange("(p j) n -> p j n", j=PACK),
                )
                for half in item[3:] or "ab":
                    raw[name + item[2] + half] = piece[:, :, 0:HALF] if item[3:] or half == "a" else piece[:, :, HALF:H]

        products_of = {"g": ["hg"], "i": ["hi", "ci"], "f": ["hf", "cf"]}
        tiles = [(gate, j) for gate in GATES for j in range(N_TILES)]
        done = set()
        grouped = {}
        codes = {}
        x_grouped = {}
        x_codes = {}
        turned_of = {}
        sums_of = {}
        biased_of = {}
        pre_of = {}
        gated_of = {}
        bias_of = {}
        cell2 = [keep.tile([P, 2, M_TILES, P], F32, name="cell%d" % j) for j in range(N_TILES // 2)]
        kept2 = [keep.tile([P, 2, M_TILES, P], F32, name="kept%d" % j) for j in range(N_TILES // 2)]
        cell = [cell2[j // 2][:, j % 2] for j in range(N_TILES)]
        kept = [kept2[j // 2][:, j % 2] for j in range(N_TILES)]
        out_rows = out.rearrange("(p m) n -> p m n", m=M_TILES)

        def regroup_part(key, engine):
            name, g, half = key[:2], int(key[2]), "ab".index(key[3])
            if key not in grouped:
                grouped[key] = regroup.tile([P, HALF, PACK], BF16, name="w_grouped", align_bytes=64)
            split = SV.get(key, SV[name])
            lo, hi = (0, split) if engine == "V" else (split, HALF)
            if lo == hi:
                return
            src = raw[key][:, :, lo:hi].rearrange("p t (c i) -> p c t i", i=4)
            dst = grouped[key][:, lo:hi].rearrange("p (c i) t -> p c t i", i=4)
            if engine == "V":
                nc.vector.tensor_copy(out=dst, in_=src)
            else:
                nc.scalar.copy(out=dst, in_=src)

        def quantise_weight(key):
            name, g = key[:2], int(key[2])
            wk = name + key[3]
            if wk not in codes:
                w_codes = quantised.tile([P, PASSES * HALF], U32, name="w_codes", align_bytes=64)
                w_scales = quantised.tile([P, PASSES * HALF], U8, name="w_scales", align_bytes=64)
                codes[wk] = (w_codes, w_scales)
            w_codes, w_scales = codes[wk]
            cols = slice(g * HALF, (g + 1) * HALF)
            nc.vector.quantize_mx(
                out=w_codes[:, cols].bitcast(FP8X4),
                scales=w_scales[:, cols],
                in_=grouped[key][:].rearrange("p c t -> p (c t)"),
            )

        def turn_x(name, k):
            g, pair = divmod(k, 2)
            turned = psum_pre.tile([P, 2, 2, P], F32, name="turned", tag="pre")
            for m in range(2):
                src = x_pair["h01" if pair == 0 else "h23"][:, m, :] if name == "h" and x_pair else rows[name][:, 2 * pair + m, :]
                words = src.bitcast(F32).rearrange("p (g q u) -> p g u q", g=PASSES, u=2)
                for u in range(2):
                    nc.tensor.transpose(turned[:, m, u, :], words[:, g, u, :], ident_f32[:])
            turned_of[name, k] = turned

        def copy_x(name, k, engine):
            g, pair = divmod(k, 2)
            if (name, g) not in x_grouped:
                x_grouped[name, g] = regroup.tile([P, B, PACK], BF16, name="x_grouped%d" % g, bufs=1, align_bytes=64)
            copy = nc.vector.tensor_copy if engine == "V" else nc.scalar.copy
            copy(
                out=x_grouped[name, g][:, pair * 2 * P : (pair + 1) * 2 * P, :].bitcast(F32).rearrange("p (m b) u -> p m b u", m=2),
                in_=turned_of[name, k][:].rearrange("p m u b -> p m b u"),
            )

        def quantise_x(name, g):
            if name not in x_codes:
                x_codes[name] = (
                    keep.tile([P, PASSES * B], U32, name=name + "_codes", align_bytes=64),
                    keep.tile([P, PASSES * B], U8, name=name + "_scales", align_bytes=64),
                )
            x_c, x_s = x_codes[name]
            nc.vector.quantize_mx(
                out=x_c[:, g * B : (g + 1) * B].bitcast(FP8X4),
                scales=x_s[:, g * B : (g + 1) * B],
                in_=x_grouped[name, g][:].rearrange("p b t -> p (b t)"),
            )

        def passes_of(t):
            return [(name, g) for name in products_of[tiles[t][0]] for g in range(PASSES)]

        def multiply(t, steps):
            gate, j = tiles[t]
            if steps[0] == 0:
                sums_of[t] = psum_sums.tile([P, B], F32, name="sums")
            sums = sums_of[t]
            half, jj = divmod(j, N_TILES // 2)
            if True:
                for step in steps:
                    name, g = passes_of(t)[step]
                    w_codes, w_scales = codes[name + "ab"[half]]
                    x_c, x_s = x_codes[name[0]]
                    w_cols = slice(g * HALF + jj * P, g * HALF + (jj + 1) * P)
                    x_cols = slice(g * B, (g + 1) * B)
                    nc.tensor.matmul_mx(
                        out=sums[:],
                        lhsT=w_codes[:, w_cols].bitcast(FP8X4),
                        lhsT_scale=w_scales[:, w_cols],
                        rhs=x_c[:, x_cols].bitcast(FP8X4),
                        rhs_scale=x_s[:, x_cols],
                        start=(step == 0),
                        stop=(step == len(passes_of(t)) - 1),
                    )

        def add_bias(t):
            biased = work.tile([P, B], F32, name="biased")
            nc.scalar.activation(
                out=biased[:], in_=sums_of[t][:], func=ACT.Identity, bias=bias_of[0][:, t : t + 1]
            )
            biased_of[t] = biased

        def open_with_xz(t):
            gate, j = tiles[t]
            pre = psum_pre.tile([P, M_TILES, P], F32, name="pre")
            nc.tensor.matmul(
                out=pre[:],
                lhsT=ident_bf16[:],
                rhs=rows["x" + gate][:, :, j * P : (j + 1) * P],
                start=True,
                stop=False,
            )
            pre_of[t] = pre

        def turn_back(t):
            for m in range(M_TILES):
                nc.tensor.matmul(
                    out=pre_of[t][:, m, :],
                    lhsT=biased_of[t][:, m * P : (m + 1) * P],
                    rhs=ident_f32[:],
                    is_transpose=True,
                    start=False,
                    stop=(m == M_TILES - 1),
                )

        def activate(t):
            gate, j = tiles[t]
            cols = slice(j * P, (j + 1) * P)
            if gate == "g":
                nc.scalar.activation(out=cell[j], in_=pre_of[t][:], func=ACT.Tanh)
            else:
                nc.scalar.activation(out=kept[j], in_=pre_of[t][:], func=ACT.Sigmoid)
                gated_of[t] = kept[j]

        def combine(t):
            gate, j = tiles[t]
            if j % 2 == 0:
                return
            if gate == "i":
                nc.vector.tensor_tensor(out=cell2[j // 2][:], in0=kept2[j // 2][:], in1=cell2[j // 2][:], op=ALU.mult)
            if gate == "f":
                k2, c2 = kept2[j // 2], cell2[j // 2]
                c_cols = rows["c"][:, :, (j - 1) * P : (j + 1) * P].rearrange("p m (j n) -> p j m n", j=2)
                if t < WIDE:
                    nc.vector.tensor_tensor(out=k2[:], in0=k2[:], in1=c_cols, op=ALU.mult)
                    nc.vector.tensor_tensor(out=k2[:], in0=k2[:], in1=c2[:], op=ALU.add)
                    for e in range(2):
                        nc.sync.dma_start(out=out_rows[:, :, (j - 1 + e) * P : (j + e) * P], in_=k2[:, e])
                else:
                    for e in range(2):
                        nc.vector.tensor_tensor(out=k2[:, e], in0=k2[:, e], in1=c_cols[:, e], op=ALU.mult)
                    for e in range(2):
                        nc.vector.tensor_tensor(out=k2[:, e], in0=k2[:, e], in1=c2[:, e], op=ALU.add)
                        nc.sync.dma_start(out=out_rows[:, :, (j - 1 + e) * P : (j + e) * P], in_=k2[:, e])

        def warm_up(count):
            idle = psum_pre.tile([P, B], F32, name="idle", tag="pre")
            for k in range(count):
                nc.tensor.matmul(out=idle[:], lhsT=ident_bf16[:], rhs=raw["hg0a"][:, k % PACK, :], start=True, stop=True)

        def bias_turn():
            bias_t = psum_pre.tile([P, P], BF16, name="bias_t", tag="pre")
            nc.tensor.transpose(bias_t[:], bias_rows[:], ident_bf16[:])
            turned_of["bias"] = bias_t

        def bias_copy():
            bias_cols = keep.tile([P, len(GATES) * N_TILES], F32, name="bias_cols")
            nc.scalar.copy(out=bias_cols[:], in_=turned_of["bias"][:, 0 : len(GATES) * N_TILES])
            bias_of[0] = bias_cols

        def vector_op(x):
            if x[0] == "K":
                t = int(x[1:])
                return ("V" + x, ["SA" + x[1:]] + (["VK%d" % (t - N_TILES)] if tiles[t][0] == "f" else []), lambda: combine(t))
            if len(x) == 2 and x[1] in "0123":
                return ("C" + x, ["P" + x], lambda: copy_x(x[0], int(x[1]), "V"))
            if x[:2] in ("qh", "qc") and len(x) == 3:
                g = int(x[2])
                return ("V" + x, ["C%s%d" % (x[1], 2 * g + e) for e in range(2)], lambda: quantise_x(x[1], g))
            if x[0] == "q":
                need = ["V" + x[1:]] + (["S" + x[1:]] if SV.get(x[1:], SV[x[1:3]]) < HALF else [])
                return ("V" + x, need, lambda: quantise_weight(x[1:]))
            return ("V" + x, [], lambda: regroup_part(x, "V"))

        def scalar_op(x):
            if x[0] == "B":
                return ("S" + x, ["PM" + x[1:], "Sbias"], lambda: add_bias(int(x[1:])))
            if x[0] == "A":
                return ("S" + x, ["PT" + x[1:]], lambda: activate(int(x[1:])))
            if x == "bias":
                return ("Sbias", ["Pbias"], bias_copy)
            if len(x) == 2:
                return ("C" + x, ["P" + x], lambda: copy_x(x[0], int(x[1]), "S"))
            return ("S" + x, [], lambda: regroup_part(x, "S"))

        def tensor_op(x):
            if x[0] == "M":
                t, part = x[1:].split(":") if ":" in x else (x[1:], "0-%d" % (len(passes_of(int(x[1:]))) - 1))
                t = int(t)
                lo, hi = part.split("-") if "-" in part else (part, part)
                steps = list(range(int(lo), int(hi) + 1))
                need = []
                for step in steps:
                    name, g = passes_of(t)[step]
                    need += ["Vq%s%d%s" % (name, g, "ab"[tiles[t][1] // 4]), "Vq%s%d" % (name[0], g)]
                last = steps[-1] == len(passes_of(t)) - 1
                return ("PM%d" % t if last else "P" + x, need, lambda: multiply(t, steps))
            if x[0] == "T":
                return ("P" + x, ["SB" + x[1:]], lambda: turn_back(int(x[1:])))
            if x[0] == "I":
                return ("P" + x, [], lambda: open_with_xz(int(x[1:])))
            if x[:2] == "dd":
                return ("P" + x, [], lambda: warm_up(int(x[2])))
            if x == "bias":
                return ("Pbias", [], bias_turn)
            return ("P" + x, [], lambda: turn_x(x[0], int(x[1])))

        def expand(order):
            flat = []
            for x in order:
                flat += [x[1] + str(m) for m in range(M_TILES)] if x in ("xh", "xc") else [x]
            return flat

        queues = [
            [vector_op(x) for x in V_ORDER],
            [scalar_op(x) for x in expand(S_ORDER)],
            [tensor_op(x) for x in expand(PE_ORDER)],
        ]
        heads = [0, 0, 0]
        moved = True
        while moved:
            moved = False
            for q in range(3):
                if heads[q] < len(queues[q]):
                    token, needs, call = queues[q][heads[q]]
                    if all(n in done for n in needs):
                        call()
                        done.add(token)
                        heads[q] += 1
                        moved = True
        assert all(heads[q] == len(queues[q]) for q in range(3)), [queues[q][heads[q]][0:2] for q in range(3) if heads[q] < len(queues[q])]
